import numpy as np
import ml_dtypes


def mxq(x, axis, fmt="e4m3"):
    dtype, down = {"e4m3": (ml_dtypes.float8_e4m3fn, 7), "e5m2": (ml_dtypes.float8_e5m2, 14)}[fmt]
    v = np.moveaxis(np.asarray(x, np.float32).astype(ml_dtypes.bfloat16).astype(np.float64), axis, -1)
    blocks = v.reshape(v.shape[:-1] + (-1, 32))
    amax = np.abs(blocks).max(-1, keepdims=True)
    byte = np.maximum(np.where(amax > 0, np.frexp(amax)[1] - 1 + 127, 0) - down, 1)
    scale = np.exp2(byte - 127.0)
    codes = (blocks / scale).astype(np.float32).astype(dtype).astype(np.float64)
    return np.moveaxis((codes * scale).reshape(v.shape), -1, axis)


WIDE = False


def mx_kscale(k):
    if not WIDE:
        return np.ones(k)
    levels = np.array([10, -10, 5, -5, 0])
    a = np.random.permutation(np.resize(levels, k // 512 * 4)).reshape(k // 512, 4)
    idx = np.arange(k)
    return np.exp2(a[idx // 512, idx % 128 // 32])


BF16 = ml_dtypes.bfloat16


def bf(x):
    return np.asarray(x, np.float32).astype(BF16)


def f64(x):
    return np.asarray(x).astype(np.float64)


E2M1 = np.array([0.0, 0.5, 1.0, 1.5, 2.0, 3.0, 4.0, 6.0, -0.0, -0.5, -1.0, -1.5, -2.0, -3.0, -4.0, -6.0])


def pack_weight(w, fmt):
    k, n = w.shape
    w = f64(bf(w)).reshape(k // 32, 32, n)
    amax = np.abs(w).max(1)
    if fmt == "e4m3":
        byte = np.frexp(amax)[1] - 1 + 127 - 7
    else:
        mant, ex = np.frexp(amax / 6.0)
        byte = np.where(mant > 0.5, ex, ex - 1) + 127
    byte = np.clip(np.where(amax > 0, byte, 1), 1, 254)
    scaled = (w * np.exp2(127.0 - byte)[:, None, :]).reshape(k, n).astype(np.float32)
    by_word = np.ascontiguousarray(scaled.reshape(k // 512, 128, 4, n).transpose(0, 1, 3, 2))
    if fmt == "e4m3":
        words = by_word.astype(ml_dtypes.float8_e4m3fn).view(np.uint8)
    else:
        c = by_word.astype(ml_dtypes.float4_e2m1fn).view(np.uint8) & 0xF
        words = c[..., 0::2] | (c[..., 1::2] << 4)
    return np.ascontiguousarray(words), np.ascontiguousarray(byte.astype(np.uint8).reshape(k // 512, 16, n))


def unpack_weight(words, scales, fmt):
    g, p, n, _ = words.shape
    if fmt == "e4m3":
        vals = np.ascontiguousarray(words).view(ml_dtypes.float8_e4m3fn).astype(np.float64)
    else:
        nib = np.empty((g, p, n, 4), np.uint8)
        nib[..., 0::2] = words & 0xF
        nib[..., 1::2] = words >> 4
        vals = E2M1[nib]
    vals = vals * np.repeat(np.exp2(scales.astype(np.float64) - 127.0), 8, axis=1)[..., None]
    return vals.transpose(0, 1, 3, 2).reshape(g * 512, n)

def pack4(w):
    words, scales = pack_weight(w, "e2m1")
    return words.reshape(words.shape[0], 128, -1), scales


def unpack4(words, scales):
    return unpack_weight(words.reshape(words.shape[0], 128, -1, 2), scales, "e2m1")


B, HW, C, HID, WS, SS, HEADS = 8, 32, 512, 2048, 8, 4, 16
L = HW * HW
NH = HW // WS
EPS = 1e-5


def adain(x, scale, shift):
    m = x.mean(2, keepdims=True)
    s = np.std(x, axis=2, keepdims=True, ddof=1) + EPS
    return (x - m) / s * scale + shift


def setup_inputs():
    s = mx_kscale(C)
    o_attn = bf(0.4 * np.random.standard_normal((NH * NH * B, WS * WS, C)) * s)
    out_w = np.random.standard_normal((C, C)) / np.sqrt(C) / s[None, :]
    words, scales = pack4(np.ascontiguousarray(out_w.T))
    return {"o_attn": o_attn,
            "out_w_words": words,
            "out_w_scales": scales,
            "out_b": bf(0.1 * np.random.standard_normal(C)),
            "ada1_scale": bf(1.0 + 0.1 * np.random.standard_normal((1, L, 1))),
            "ada1_shift": bf(0.1 * np.random.standard_normal((1, L, 1))),
            "x": bf(np.random.standard_normal((B, L, C)))}


def reference(o_attn, out_w_words, out_w_scales, out_b, ada1_scale, ada1_shift, x):
    a = (mxq(f64(o_attn), 2, "e4m3") @ unpack4(out_w_words, out_w_scales)) + f64(out_b)
    a = np.swapaxes(a.reshape(B, NH, NH, WS, WS, C), 2, 3).reshape(B, HW, HW, C)
    a = np.roll(a, (SS, SS), axis=(1, 2)).reshape(B, L, C)
    return f64(x) + adain(a, f64(ada1_scale), f64(ada1_shift))

@@ -1,0 +1,240 @@
+from contextlib import ExitStack
+
+import concourse.mybir as mybir
+from concourse.masks import make_identity
+
+F32 = mybir.dt.float32
+BF16 = mybir.dt.bfloat16
+I32 = mybir.dt.int32
+U32 = mybir.dt.uint32
+U8 = mybir.dt.uint8
+FP8X4 = mybir.dt.float8_e4m3fn_x4
+FP4X4 = mybir.dt.float4_e2m1fn_x4
+ALU = mybir.AluOpType
+ACT = mybir.ActivationFunctionType
+
+P = 128
+C = 512
+IMAGES = 8
+RUN = 8
+TILES = 4
+GROUPS = IMAGES * RUN // TILES
+EPS = 1e-5
+
+FLOPS = 2 * IMAGES * 1024 * C * C
+
+MATMUL_AHEAD = 1
+QUANTISE_AHEAD = 2
+TRANSPOSE_AHEAD = 3
+O_LOAD_AHEAD = 5
+X_LOAD_AHEAD = 3
+
+
+def tile_swintransformerblock_pb_t_kernel(
+    tc, o_attn, out_w_words, out_w_scales, out_b, ada1_scale, ada1_shift, x, out
+):
+    nc = tc.nc
+
+    o_rows = o_attn.rearrange("w (r c) k -> (w r) c k", c=RUN)
+    x_rows = x.rearrange("b (m t) k -> b m t k", t=RUN)
+    out_rows = out.rearrange("b (m t) k -> b m t k", t=RUN)
+
+    with ExitStack() as ctx:
+        ctx.enter_context(tc.manual_schedule())
+        const = ctx.enter_context(tc.tile_pool(name="const", bufs=1))
+        o_pool = ctx.enter_context(tc.tile_pool(name="o", bufs=4))
+        x_pool = ctx.enter_context(tc.tile_pool(name="x", bufs=5))
+        mx_pool = ctx.enter_context(tc.tile_pool(name="mx", bufs=3))
+        work = ctx.enter_context(tc.tile_pool(name="work", bufs=3))
+        stats = ctx.enter_context(tc.tile_pool(name="stats", bufs=3))
+        tp_pool = ctx.enter_context(tc.psum_pool(name="tp", bufs=4))
+        y_pool = ctx.enter_context(tc.psum_pool(name="y", bufs=4))
+
+        o_of, x_of, grouped_of, codes_of, scales_of, y_of = {}, {}, {}, {}, {}, {}
+        a_of, sums_of, negmean_of, std_of, gain_of, offset_of, shifted_of = {}, {}, {}, {}, {}, {}, {}
+
+        def place(g):
+            b, hc = divmod(g, 2)
+            return b, hc, 1 - hc
+
+        def load_o(g):
+            b, hc, ht = place(g)
+            o_sb = o_pool.tile([P, TILES, C], BF16)
+            nc.sync.dma_start(out=o_sb[:], in_=o_rows[P * b : P * (b + 1), TILES * hc : TILES * (hc + 1), :])
+            o_of[g] = o_sb
+
+        def load_x(g):
+            b, hc, ht = place(g)
+            x_sb = x_pool.tile([P, TILES, C], BF16)
+            nc.sync.dma_start(out=x_sb[:], in_=x_rows[b, :, TILES * ht : TILES * (ht + 1), :])
+            x_of[g] = x_sb
+
+        load_o(0)
+
+        w_words = const.tile([P, 2 * C], U8, align_bytes=64)
+        w_scales = const.tile([P, C], U8, align_bytes=64)
+        nc.vector.memset(w_scales[:].bitcast(I32), 0)
+        nc.sync.dma_start(out=w_words[:].bitcast(I32), in_=out_w_words[0].bitcast(I32))
+        for quadrant in range(4):
+            nc.sync.dma_start(
+                out=w_scales[32 * quadrant : 32 * quadrant + 4, :].bitcast(I32),
+                in_=out_w_scales[0, 4 * quadrant : 4 * quadrant + 4, :].bitcast(I32),
+            )
+        for g in range(1, O_LOAD_AHEAD - TRANSPOSE_AHEAD):
+            load_o(g)
+
+        bias_sb = const.tile([P, C], BF16)
+        nc.scalar.dma_start(out=bias_sb[:], in_=out_b.partition_broadcast(P))
+        ada_scale_sb = const.tile([P, RUN], BF16)
+        nc.scalar.dma_start(out=ada_scale_sb[:], in_=ada1_scale[0].rearrange("(m t) u -> m (t u)", t=RUN))
+        ada_shift_sb = const.tile([P, RUN], BF16)
+        nc.scalar.dma_start(out=ada_shift_sb[:], in_=ada1_shift[0].rearrange("(m t) u -> m (t u)", t=RUN))
+
+        ident = const.tile([P, P], F32)
+        make_identity(nc, ident[:])
+        perm_lo = const.tile([P, P], F32)
+        nc.vector.tensor_copy(
+            out=perm_lo[:, 16:112].rearrange("q (wi r j) -> q wi r j", wi=3, r=8),
+            in_=ident[:, 0:96].rearrange("q (wi j r) -> q wi r j", wi=3, j=4),
+        )
+        last_windows = ident[:, 96:128].rearrange("q (j r) -> q r j", j=4)
+        nc.vector.tensor_copy(out=perm_lo[:, 112:128].rearrange("q (r j) -> q r j", r=4), in_=last_windows[:, 0:4, :])
+        nc.vector.tensor_copy(out=perm_lo[:, 0:16].rearrange("q (r j) -> q r j", r=4), in_=last_windows[:, 4:8, :])
+        perm_hi = const.tile([P, P], F32)
+        lo_ij = perm_lo[:].rearrange("q (i j) -> q i j", j=4)
+        hi_ij = perm_hi[:].rearrange("q (i j) -> q i j", j=4)
+        nc.vector.tensor_copy(out=hi_ij[:, :, 1:4], in_=lo_ij[:, :, 0:3])
+        nc.vector.tensor_copy(out=hi_ij[:, :, 0:1], in_=lo_ij[:, :, 3:4])
+        perm = [perm_lo, perm_hi]
+
+        squares = const.tile([P, C], BF16)
+
+        def transpose_and_regroup(g):
+            b, hc, ht = place(g)
+            o_words = o_of[g][:].bitcast(F32)
+            grouped = mx_pool.tile([P, TILES * P * 4], BF16, align_bytes=64)
+            grouped_words = grouped[:].bitcast(F32).rearrange("p (n u) -> p n u", u=2)
+            for pair in range(TILES // 2):
+                tp = tp_pool.tile([P, 2, 2 * P], F32)
+                for half in range(2):
+                    for u in range(2):
+                        nc.tensor.transpose(
+                            tp[:, u, P * half : P * (half + 1)],
+                            o_words[:, 2 * pair + half, u : C // 2 : 2],
+                            perm[hc][:],
+                        )
+                nc.scalar.copy(
+                    out=grouped_words[:, 2 * P * pair : 2 * P * (pair + 1), :],
+                    in_=tp[:].rearrange("p u n -> p n u"),
+                )
+            grouped_of[g] = grouped
+
+        def quantise(g):
+            codes = mx_pool.tile([P, TILES * P], U32, align_bytes=64)
+            scales = mx_pool.tile([P, TILES * P], U8, align_bytes=64)
+            nc.vector.quantize_mx(out=codes[:].bitcast(FP8X4), scales=scales[:], in_=grouped_of[g][:])
+            codes_of[g], scales_of[g] = codes, scales
+
+        def project(g):
+            y_of[g] = []
+            for j in range(TILES):
+                y = y_pool.tile([P, C], F32)
+                nc.tensor.matmul_mx(
+                    out=y[:],
+                    lhsT=codes_of[g][:, P * j : P * (j + 1)].bitcast(FP8X4),
+                    lhsT_scale=scales_of[g][:, P * j : P * (j + 1)],
+                    rhs=w_words[:].bitcast(FP4X4),
+                    rhs_scale=w_scales[:],
+                    start=True,
+                    stop=True,
+                )
+                y_of[g].append(y)
+
+        def add_bias(g):
+            a = work.tile([P, TILES, C], F32)
+            sums = stats.tile([P, TILES], F32)
+            for j in range(TILES):
+                nc.vector.scalar_tensor_tensor(
+                    out=a[:, j, :],
+                    in0=y_of[g][j][:],
+                    scalar=1.0,
+                    in1=bias_sb[:],
+                    op0=ALU.mult,
+                    op1=ALU.add,
+                    accum_out=sums[:, j : j + 1],
+                )
+            negmean = stats.tile([P, TILES], F32)
+            nc.vector.tensor_scalar_mul(out=negmean[:], in0=sums[:], scalar1=-1.0 / C)
+            a_of[g], negmean_of[g] = a, negmean
+
+        def deviation(g):
+            sumsq = stats.tile([P, TILES], F32)
+            for j in range(TILES):
+                nc.scalar.activation(
+                    out=squares[:],
+                    in_=a_of[g][:, j, :],
+                    func=ACT.Square,
+                    bias=negmean_of[g][:, j : j + 1],
+                    scale=1.0,
+                    accum_out=sumsq[:, j : j + 1],
+                )
+            std = stats.tile([P, TILES], F32)
+            nc.scalar.activation(out=std[:], in_=sumsq[:], func=ACT.Sqrt, scale=1.0 / (C - 1))
+            std_of[g] = std
+
+        def gain_and_offset(g):
+            b, hc, ht = place(g)
+            tiles_of_image = slice(TILES * ht, TILES * (ht + 1))
+            denom = stats.tile([P, TILES], F32)
+            nc.vector.tensor_scalar_add(out=denom[:], in0=std_of[g][:], scalar1=EPS)
+            recip = stats.tile([P, TILES], F32)
+            nc.vector.reciprocal(out=recip[:], in_=denom[:])
+            gain = stats.tile([P, TILES], F32)
+            nc.vector.tensor_mul(out=gain[:], in0=recip[:], in1=ada_scale_sb[:, tiles_of_image])
+            centre = stats.tile([P, TILES], F32)
+            nc.vector.tensor_mul(out=centre[:], in0=negmean_of[g][:], in1=gain[:])
+            offset = stats.tile([P, TILES], F32)
+            nc.vector.tensor_add(out=offset[:], in0=centre[:], in1=ada_shift_sb[:, tiles_of_image])
+            gain_of[g], offset_of[g] = gain, offset
+
+        def shift_x(g):
+            shifted = work.tile([P, TILES, C], F32)
+            for j in range(TILES):
+                nc.scalar.activation(
+                    out=shifted[:, j, :],
+                    in_=x_of[g][:, j, :],
+                    func=ACT.Identity,
+                    bias=offset_of[g][:, j : j + 1],
+                    scale=1.0,
+                )
+            shifted_of[g] = shifted
+
+        def finish(g):
+            b, hc, ht = place(g)
+            result = work.tile([P, TILES, C], F32)
+            for j in range(TILES):
+                nc.vector.scalar_tensor_tensor(
+                    out=result[:, j, :],
+                    in0=a_of[g][:, j, :],
+                    scalar=gain_of[g][:, j : j + 1],
+                    in1=shifted_of[g][:, j, :],
+                    op0=ALU.mult,
+                    op1=ALU.add,
+                )
+            nc.sync.dma_start(out=out_rows[b, :, TILES * ht : TILES * (ht + 1), :], in_=result[:])
+
+        def run(stage, g):
+            if 0 <= g < GROUPS:
+                stage(g)
+
+        for i in range(-TRANSPOSE_AHEAD, GROUPS + 1):
+            run(load_o, i + O_LOAD_AHEAD)
+            run(load_x, i + X_LOAD_AHEAD)
+            run(shift_x, i - 1)
+            run(add_bias, i)
+            run(project, i + MATMUL_AHEAD)
+            run(deviation, i)
+            run(finish, i - 1)
+            run(transpose_and_regroup, i + TRANSPOSE_AHEAD)
+            run(quantise, i + QUANTISE_AHEAD)
+            run(gain_and_offset, i)

@@ -227,14 +227,14 @@ def tile_swintransformerblock_pb_t_kernel(
             if 0 <= g < GROUPS:
                 stage(g)
 
-        for i in range(-TRANSPOSE_AHEAD, GROUPS + 1):
+        for i in range(-TRANSPOSE_AHEAD, GROUPS + 2):
             run(load_o, i + O_LOAD_AHEAD)
             run(load_x, i + X_LOAD_AHEAD)
-            run(shift_x, i - 1)
             run(add_bias, i)
             run(project, i + MATMUL_AHEAD)
+            run(gain_and_offset, i - 1)
             run(deviation, i)
-            run(finish, i - 1)
             run(transpose_and_regroup, i + TRANSPOSE_AHEAD)
+            run(shift_x, i - 1)
+            run(finish, i - 2)
             run(quantise, i + QUANTISE_AHEAD)
-            run(gain_and_offset, i)

@@ -51,7 +51,8 @@ def tile_swintransformerblock_pb_t_kernel(
         y_pool = ctx.enter_context(tc.psum_pool(name="y", bufs=4))
 
         o_of, x_of, grouped_of, codes_of, scales_of, y_of = {}, {}, {}, {}, {}, {}
-        a_of, sums_of, negmean_of, std_of, gain_of, offset_of, shifted_of = {}, {}, {}, {}, {}, {}, {}
+        a_of, negmean_of, sumsq_of, std_of, gain_of, offset_of, shifted_of = {}, {}, {}, {}, {}, {}, {}
+        tp_of, denom_of, recip_of, centre_of, result_of = {}, {}, {}, {}, {}
 
         def place(g):
             b, hc = divmod(g, 2)
@@ -109,25 +110,33 @@ def tile_swintransformerblock_pb_t_kernel(
 
         squares = const.tile([P, C], BF16)
 
-        def transpose_and_regroup(g):
+        bias_s = const.tile([P, C], F32)
+        nc.vector.tensor_scalar_mul(out=bias_s[:], in0=bias_sb[:], scalar1=-1.0 / C)
+        ada_scale_s = const.tile([P, RUN], F32)
+        nc.vector.tensor_scalar_mul(out=ada_scale_s[:], in0=ada_scale_sb[:], scalar1=-1.0 * C)
+
+        def transposes(g, pair):
             b, hc, ht = place(g)
             o_words = o_of[g][:].bitcast(F32)
-            grouped = mx_pool.tile([P, TILES * P * 4], BF16, align_bytes=64)
-            grouped_words = grouped[:].bitcast(F32).rearrange("p (n u) -> p n u", u=2)
-            for pair in range(TILES // 2):
-                tp = tp_pool.tile([P, 2, 2 * P], F32)
-                for half in range(2):
-                    for u in range(2):
-                        nc.tensor.transpose(
-                            tp[:, u, P * half : P * (half + 1)],
-                            o_words[:, 2 * pair + half, u : C // 2 : 2],
-                            perm[hc][:],
-                        )
-                nc.scalar.copy(
-                    out=grouped_words[:, 2 * P * pair : 2 * P * (pair + 1), :],
-                    in_=tp[:].rearrange("p u n -> p n u"),
-                )
-            grouped_of[g] = grouped
+            tp = tp_pool.tile([P, 2, 2 * P], F32)
+            for half in range(2):
+                for u in range(2):
+                    nc.tensor.transpose(
+                        tp[:, u, P * half : P * (half + 1)],
+                        o_words[:, 2 * pair + half, u : C // 2 : 2],
+                        perm[hc][:],
+                    )
+            tp_of[g, pair] = tp
+
+        def regroup(g, pair):
+            if pair == 0:
+                grouped = mx_pool.tile([P, TILES * P * 4], BF16, align_bytes=64)
+                grouped_of[g] = grouped
+            grouped_words = grouped_of[g][:].bitcast(F32).rearrange("p (n u) -> p n u", u=2)
+            nc.scalar.copy(
+                out=grouped_words[:, 2 * P * pair : 2 * P * (pair + 1), :],
+                in_=tp_of[g, pair][:].rearrange("p u n -> p n u"),
+            )
 
         def quantise(g):
             codes = mx_pool.tile([P, TILES * P], U32, align_bytes=64)
@@ -135,106 +144,134 @@ def tile_swintransformerblock_pb_t_kernel(
             nc.vector.quantize_mx(out=codes[:].bitcast(FP8X4), scales=scales[:], in_=grouped_of[g][:])
             codes_of[g], scales_of[g] = codes, scales
 
-        def project(g):
-            y_of[g] = []
-            for j in range(TILES):
-                y = y_pool.tile([P, C], F32)
-                nc.tensor.matmul_mx(
-                    out=y[:],
-                    lhsT=codes_of[g][:, P * j : P * (j + 1)].bitcast(FP8X4),
-                    lhsT_scale=scales_of[g][:, P * j : P * (j + 1)],
-                    rhs=w_words[:].bitcast(FP4X4),
-                    rhs_scale=w_scales[:],
-                    start=True,
-                    stop=True,
-                )
-                y_of[g].append(y)
+        def project(g, j):
+            y = y_pool.tile([P, C], F32)
+            nc.tensor.matmul_mx(
+                out=y[:],
+                lhsT=codes_of[g][:, P * j : P * (j + 1)].bitcast(FP8X4),
+                lhsT_scale=scales_of[g][:, P * j : P * (j + 1)],
+                rhs=w_words[:].bitcast(FP4X4),
+                rhs_scale=w_scales[:],
+                start=True,
+                stop=True,
+            )
+            y_of[g, j] = y
 
-        def add_bias(g):
-            a = work.tile([P, TILES, C], F32)
-            sums = stats.tile([P, TILES], F32)
-            for j in range(TILES):
-                nc.vector.scalar_tensor_tensor(
-                    out=a[:, j, :],
-                    in0=y_of[g][j][:],
-                    scalar=1.0,
-                    in1=bias_sb[:],
-                    op0=ALU.mult,
-                    op1=ALU.add,
-                    accum_out=sums[:, j : j + 1],
-                )
-            negmean = stats.tile([P, TILES], F32)
-            nc.vector.tensor_scalar_mul(out=negmean[:], in0=sums[:], scalar1=-1.0 / C)
-            a_of[g], negmean_of[g] = a, negmean
+        def add_bias(g, j):
+            if j == 0:
+                a = work.tile([P, TILES, C], F32)
+                negmean = stats.tile([P, TILES], F32)
+                a_of[g], negmean_of[g] = a, negmean
+            nc.vector.scalar_tensor_tensor(
+                out=a_of[g][:, j, :],
+                in0=y_of[g, j][:],
+                scalar=-1.0 / C,
+                in1=bias_s[:],
+                op0=ALU.mult,
+                op1=ALU.add,
+                accum_out=negmean_of[g][:, j : j + 1],
+            )
 
-        def deviation(g):
-            sumsq = stats.tile([P, TILES], F32)
-            for j in range(TILES):
-                nc.scalar.activation(
-                    out=squares[:],
-                    in_=a_of[g][:, j, :],
-                    func=ACT.Square,
-                    bias=negmean_of[g][:, j : j + 1],
-                    scale=1.0,
-                    accum_out=sumsq[:, j : j + 1],
-                )
+        def square(g, j):
+            if j == 0:
+                sumsq = stats.tile([P, TILES], F32)
+                sumsq_of[g] = sumsq
+            nc.scalar.activation(
+                out=squares[:],
+                in_=a_of[g][:, j, :],
+                func=ACT.Square,
+                bias=negmean_of[g][:, j : j + 1],
+                scale=-1.0 * C,
+                accum_out=sumsq_of[g][:, j : j + 1],
+            )
+
+        def root(g):
             std = stats.tile([P, TILES], F32)
-            nc.scalar.activation(out=std[:], in_=sumsq[:], func=ACT.Sqrt, scale=1.0 / (C - 1))
+            nc.scalar.activation(out=std[:], in_=sumsq_of[g][:], func=ACT.Sqrt, scale=1.0 / (C - 1))
             std_of[g] = std
 
-        def gain_and_offset(g):
+        def chain(g, step):
             b, hc, ht = place(g)
             tiles_of_image = slice(TILES * ht, TILES * (ht + 1))
-            denom = stats.tile([P, TILES], F32)
-            nc.vector.tensor_scalar_add(out=denom[:], in0=std_of[g][:], scalar1=EPS)
-            recip = stats.tile([P, TILES], F32)
-            nc.vector.reciprocal(out=recip[:], in_=denom[:])
-            gain = stats.tile([P, TILES], F32)
-            nc.vector.tensor_mul(out=gain[:], in0=recip[:], in1=ada_scale_sb[:, tiles_of_image])
-            centre = stats.tile([P, TILES], F32)
-            nc.vector.tensor_mul(out=centre[:], in0=negmean_of[g][:], in1=gain[:])
-            offset = stats.tile([P, TILES], F32)
-            nc.vector.tensor_add(out=offset[:], in0=centre[:], in1=ada_shift_sb[:, tiles_of_image])
-            gain_of[g], offset_of[g] = gain, offset
-
-        def shift_x(g):
-            shifted = work.tile([P, TILES, C], F32)
-            for j in range(TILES):
-                nc.scalar.activation(
-                    out=shifted[:, j, :],
-                    in_=x_of[g][:, j, :],
-                    func=ACT.Identity,
-                    bias=offset_of[g][:, j : j + 1],
-                    scale=1.0,
-                )
-            shifted_of[g] = shifted
-
-        def finish(g):
-            b, hc, ht = place(g)
-            result = work.tile([P, TILES, C], F32)
-            for j in range(TILES):
+            if step == 0:
+                denom = stats.tile([P, TILES], F32)
+                nc.vector.tensor_scalar_add(out=denom[:], in0=std_of[g][:], scalar1=EPS)
+                denom_of[g] = denom
+            elif step == 1:
+                recip = stats.tile([P, TILES], F32)
+                nc.vector.reciprocal(out=recip[:], in_=denom_of[g][:])
+                recip_of[g] = recip
+            elif step == 2:
+                gain = stats.tile([P, TILES], F32)
+                nc.vector.tensor_mul(out=gain[:], in0=recip_of[g][:], in1=ada_scale_s[:, tiles_of_image])
+                gain_of[g] = gain
+            elif step == 3:
+                centre = stats.tile([P, TILES], F32)
                 nc.vector.scalar_tensor_tensor(
-                    out=result[:, j, :],
-                    in0=a_of[g][:, j, :],
-                    scalar=gain_of[g][:, j : j + 1],
-                    in1=shifted_of[g][:, j, :],
+                    out=centre[:],
+                    in0=negmean_of[g][:],
+                    scalar=-1.0 / C,
+                    in1=gain_of[g][:],
                     op0=ALU.mult,
-                    op1=ALU.add,
+                    op1=ALU.mult,
                 )
-            nc.sync.dma_start(out=out_rows[b, :, TILES * ht : TILES * (ht + 1), :], in_=result[:])
+                centre_of[g] = centre
+            else:
+                offset = stats.tile([P, TILES], F32)
+                nc.vector.tensor_add(out=offset[:], in0=centre_of[g][:], in1=ada_shift_sb[:, tiles_of_image])
+                offset_of[g] = offset
 
-        def run(stage, g):
+        def shift_x(g, j):
+            if j == 0:
+                shifted = work.tile([P, TILES, C], F32)
+                shifted_of[g] = shifted
+            nc.scalar.activation(
+                out=shifted_of[g][:, j, :],
+                in_=x_of[g][:, j, :],
+                func=ACT.Identity,
+                bias=offset_of[g][:, j : j + 1],
+                scale=1.0,
+            )
+
+        def finish(g, j):
+            b, hc, ht = place(g)
+            if j == 0:
+                result = work.tile([P, TILES, C], F32)
+                result_of[g] = result
+            nc.vector.scalar_tensor_tensor(
+                out=result_of[g][:, j, :],
+                in0=a_of[g][:, j, :],
+                scalar=gain_of[g][:, j : j + 1],
+                in1=shifted_of[g][:, j, :],
+                op0=ALU.mult,
+                op1=ALU.add,
+            )
+            if j == TILES - 1:
+                nc.sync.dma_start(out=out_rows[b, :, TILES * ht : TILES * (ht + 1), :], in_=result_of[g][:])
+
+        def run(stage, g, *args):
             if 0 <= g < GROUPS:
-                stage(g)
+                stage(g, *args)
 
         for i in range(-TRANSPOSE_AHEAD, GROUPS + 2):
             run(load_o, i + O_LOAD_AHEAD)
             run(load_x, i + X_LOAD_AHEAD)
-            run(add_bias, i)
-            run(project, i + MATMUL_AHEAD)
-            run(gain_and_offset, i - 1)
-            run(deviation, i)
-            run(transpose_and_regroup, i + TRANSPOSE_AHEAD)
-            run(shift_x, i - 1)
-            run(finish, i - 2)
+            for pair in range(TILES // 2):
+                run(transposes, i + TRANSPOSE_AHEAD, pair)
+            for j in range(TILES):
+                run(add_bias, i, j)
+                run(chain, i - 1, j)
+            for j in range(TILES):
+                run(project, i + MATMUL_AHEAD, j)
+            for j in range(TILES):
+                run(finish, i - 2, j)
+                if j == 0:
+                    run(chain, i - 1, 4)
             run(quantise, i + QUANTISE_AHEAD)
+            for j in range(TILES):
+                run(square, i, j)
+            run(root, i)
+            for pair in range(TILES // 2):
+                run(regroup, i + TRANSPOSE_AHEAD, pair)
+            for j in range(TILES):
+                run(shift_x, i - 1, j)

@@ -233,6 +233,11 @@ def tile_swintransformerblock_pb_t_kernel(
                 scale=1.0,
             )
 
+        def shift_x_on_vector(g, j):
+            nc.vector.tensor_scalar_add(
+                out=shifted_of[g][:, j, :], in0=x_of[g][:, j, :], scalar1=offset_of[g][:, j : j + 1]
+            )
+
         def finish(g, j):
             b, hc, ht = place(g)
             if j == 0:
@@ -263,15 +268,17 @@ def tile_swintransformerblock_pb_t_kernel(
                 run(chain, i - 1, j)
             for j in range(TILES):
                 run(project, i + MATMUL_AHEAD, j)
-            for j in range(TILES):
-                run(finish, i - 2, j)
-                if j == 0:
-                    run(chain, i - 1, 4)
-            run(quantise, i + QUANTISE_AHEAD)
+            run(finish, i - 2, 0)
+            run(chain, i - 1, 4)
+            run(finish, i - 2, 1)
             for j in range(TILES):
                 run(square, i, j)
             run(root, i)
             for pair in range(TILES // 2):
                 run(regroup, i + TRANSPOSE_AHEAD, pair)
-            for j in range(TILES):
+            for j in range(TILES - 1):
                 run(shift_x, i - 1, j)
+            run(shift_x_on_vector, i - 1, TILES - 1)
+            run(finish, i - 2, 2)
+            run(finish, i - 2, 3)
+            run(quantise, i + QUANTISE_AHEAD)

@@ -273,9 +273,9 @@ def tile_swintransformerblock_pb_t_kernel(
             run(finish, i - 2, 1)
             for j in range(TILES):
                 run(square, i, j)
+            run(regroup, i + TRANSPOSE_AHEAD, 0)
             run(root, i)
-            for pair in range(TILES // 2):
-                run(regroup, i + TRANSPOSE_AHEAD, pair)
+            run(regroup, i + TRANSPOSE_AHEAD, 1)
             for j in range(TILES - 1):
                 run(shift_x, i - 1, j)
             run(shift_x_on_vector, i - 1, TILES - 1)

@@ -108,7 +108,7 @@ def tile_swintransformerblock_pb_t_kernel(
         nc.vector.tensor_copy(out=hi_ij[:, :, 0:1], in_=lo_ij[:, :, 3:4])
         perm = [perm_lo, perm_hi]
 
-        squares = const.tile([P, C], BF16)
+        squares = const.tile([P, TILES, C], BF16)
 
         bias_s = const.tile([P, C], F32)
         nc.vector.tensor_scalar_mul(out=bias_s[:], in0=bias_sb[:], scalar1=-1.0 / C)
@@ -177,7 +177,7 @@ def tile_swintransformerblock_pb_t_kernel(
                 sumsq = stats.tile([P, TILES], F32)
                 sumsq_of[g] = sumsq
             nc.scalar.activation(
-                out=squares[:],
+                out=squares[:, j, :],
                 in_=a_of[g][:, j, :],
                 func=ACT.Square,
                 bias=negmean_of[g][:, j : j + 1],

@@ -43,7 +43,7 @@ def tile_swintransformerblock_pb_t_kernel(
         ctx.enter_context(tc.manual_schedule())
         const = ctx.enter_context(tc.tile_pool(name="const", bufs=1))
         o_pool = ctx.enter_context(tc.tile_pool(name="o", bufs=4))
-        x_pool = ctx.enter_context(tc.tile_pool(name="x", bufs=5))
+        x_pool = ctx.enter_context(tc.tile_pool(name="x", bufs=6))
         mx_pool = ctx.enter_context(tc.tile_pool(name="mx", bufs=3))
         work = ctx.enter_context(tc.tile_pool(name="work", bufs=3))
         stats = ctx.enter_context(tc.tile_pool(name="stats", bufs=3))
@@ -233,6 +233,16 @@ def tile_swintransformerblock_pb_t_kernel(
                 scale=1.0,
             )
 
+        def shift_x_on_gpsimd(g, j):
+            nc.gpsimd.tensor_scalar(
+                out=shifted_of[g][:, j, :],
+                in0=x_of[g][:, j, :],
+                scalar1=1.0,
+                scalar2=offset_of[g][:, j : j + 1],
+                op0=ALU.mult,
+                op1=ALU.add,
+            )
+
         def shift_x_on_vector(g, j):
             nc.vector.tensor_scalar_add(
                 out=shifted_of[g][:, j, :], in0=x_of[g][:, j, :], scalar1=offset_of[g][:, j : j + 1]
@@ -263,22 +273,22 @@ def tile_swintransformerblock_pb_t_kernel(
             run(load_x, i + X_LOAD_AHEAD)
             for pair in range(TILES // 2):
                 run(transposes, i + TRANSPOSE_AHEAD, pair)
+            run(shift_x, i - 2, 0)
+            run(shift_x, i - 2, 1)
+            helper = shift_x_on_gpsimd if i < GROUPS else shift_x_on_vector
+            run(helper, i - 2, 2)
+            run(helper, i - 2, 3)
             for j in range(TILES):
                 run(add_bias, i, j)
-                run(chain, i - 1, j)
             for j in range(TILES):
                 run(project, i + MATMUL_AHEAD, j)
-            run(finish, i - 2, 0)
-            run(chain, i - 1, 4)
-            run(finish, i - 2, 1)
             for j in range(TILES):
                 run(square, i, j)
             run(regroup, i + TRANSPOSE_AHEAD, 0)
             run(root, i)
             run(regroup, i + TRANSPOSE_AHEAD, 1)
-            for j in range(TILES - 1):
-                run(shift_x, i - 1, j)
-            run(shift_x_on_vector, i - 1, TILES - 1)
-            run(finish, i - 2, 2)
-            run(finish, i - 2, 3)
+            for j in range(TILES):
+                run(finish, i - 2, j)
+                run(chain, i - 1, j)
             run(quantise, i + QUANTISE_AHEAD)
+            run(chain, i - 1, 4)

@@ -61,7 +61,12 @@ def tile_swintransformerblock_pb_t_kernel(
         def load_o(g):
             b, hc, ht = place(g)
             o_sb = o_pool.tile([P, TILES, C], BF16)
-            nc.sync.dma_start(out=o_sb[:], in_=o_rows[P * b : P * (b + 1), TILES * hc : TILES * (hc + 1), :])
+            step = TILES // 2 if g == 0 else TILES
+            for j in range(0, TILES, step):
+                nc.sync.dma_start(
+                    out=o_sb[:, j : j + step, :],
+                    in_=o_rows[P * b : P * (b + 1), TILES * hc + j : TILES * hc + j + step, :],
+                )
             o_of[g] = o_sb
 
         def load_x(g):
@@ -84,8 +89,11 @@ def tile_swintransformerblock_pb_t_kernel(
         for g in range(1, O_LOAD_AHEAD - TRANSPOSE_AHEAD):
             load_o(g)
 
-        bias_sb = const.tile([P, C], BF16)
-        nc.scalar.dma_start(out=bias_sb[:], in_=out_b.partition_broadcast(P))
+        bias_row = const.tile([P, C], BF16)
+        nc.vector.memset(bias_row[:], 0.0)
+        nc.scalar.dma_start(out=bias_row[0:1, :], in_=out_b.rearrange("(u c) -> u c", u=1))
+        ones = const.tile([P, P], BF16)
+        nc.vector.memset(ones[:], 1.0)
         ada_scale_sb = const.tile([P, RUN], BF16)
         nc.scalar.dma_start(out=ada_scale_sb[:], in_=ada1_scale[0].rearrange("(m t) u -> m (t u)", t=RUN))
         ada_shift_sb = const.tile([P, RUN], BF16)
@@ -111,9 +119,15 @@ def tile_swintransformerblock_pb_t_kernel(
         squares = const.tile([P, TILES, C], BF16)
 
         bias_s = const.tile([P, C], F32)
-        nc.vector.tensor_scalar_mul(out=bias_s[:], in0=bias_sb[:], scalar1=-1.0 / C)
         ada_scale_s = const.tile([P, RUN], F32)
-        nc.vector.tensor_scalar_mul(out=ada_scale_s[:], in0=ada_scale_sb[:], scalar1=-1.0 * C)
+        bias_ps = y_pool.tile([P, C], F32, tag="y")
+
+        def spread_bias():
+            nc.tensor.matmul(out=bias_ps[:], lhsT=ones[:], rhs=bias_row[:], start=True, stop=True)
+
+        def scale_constants():
+            nc.vector.tensor_scalar_mul(out=bias_s[:], in0=bias_ps[:], scalar1=-1.0 / C)
+            nc.vector.tensor_scalar_mul(out=ada_scale_s[:], in0=ada_scale_sb[:], scalar1=-1.0 * C)
 
         def transposes(g, pair):
             b, hc, ht = place(g)
@@ -141,11 +155,17 @@ def tile_swintransformerblock_pb_t_kernel(
         def quantise(g):
             codes = mx_pool.tile([P, TILES * P], U32, align_bytes=64)
             scales = mx_pool.tile([P, TILES * P], U8, align_bytes=64)
-            nc.vector.quantize_mx(out=codes[:].bitcast(FP8X4), scales=scales[:], in_=grouped_of[g][:])
+            width = TILES * P // 2 if g == 0 else TILES * P
+            for n in range(0, TILES * P, width):
+                nc.vector.quantize_mx(
+                    out=codes[:, n : n + width].bitcast(FP8X4),
+                    scales=scales[:, n : n + width],
+                    in_=grouped_of[g][:, 4 * n : 4 * (n + width)],
+                )
             codes_of[g], scales_of[g] = codes, scales
 
         def project(g, j):
-            y = y_pool.tile([P, C], F32)
+            y = y_pool.tile([P, C], F32, tag="y")
             nc.tensor.matmul_mx(
                 out=y[:],
                 lhsT=codes_of[g][:, P * j : P * (j + 1)].bitcast(FP8X4),
@@ -221,12 +241,15 @@ def tile_swintransformerblock_pb_t_kernel(
                 nc.vector.tensor_add(out=offset[:], in0=centre_of[g][:], in1=ada_shift_sb[:, tiles_of_image])
                 offset_of[g] = offset
 
-        def shift_x(g, j):
-            if j == 0:
+        def shifted_tile(g):
+            if g not in shifted_of:
                 shifted = work.tile([P, TILES, C], F32)
                 shifted_of[g] = shifted
+            return shifted_of[g]
+
+        def shift_x(g, j):
             nc.scalar.activation(
-                out=shifted_of[g][:, j, :],
+                out=shifted_tile(g)[:, j, :],
                 in_=x_of[g][:, j, :],
                 func=ACT.Identity,
                 bias=offset_of[g][:, j : j + 1],
@@ -248,21 +271,42 @@ def tile_swintransformerblock_pb_t_kernel(
                 out=shifted_of[g][:, j, :], in0=x_of[g][:, j, :], scalar1=offset_of[g][:, j : j + 1]
             )
 
-        def finish(g, j):
-            b, hc, ht = place(g)
-            if j == 0:
+        def result_tile(g):
+            if g not in result_of:
                 result = work.tile([P, TILES, C], F32)
                 result_of[g] = result
+            return result_of[g]
+
+        def scale_a(g, j):
+            nc.scalar.activation(
+                out=shifted_tile(g)[:, j, :],
+                in_=a_of[g][:, j, :],
+                func=ACT.Identity,
+                bias=offset_of[g][:, j : j + 1],
+                scale=gain_of[g][:, j : j + 1],
+            )
+
+        def add_x_on_gpsimd(g, j):
+            nc.gpsimd.tensor_tensor(
+                out=result_tile(g)[:, j, :], in0=shifted_of[g][:, j, :], in1=x_of[g][:, j, :], op=ALU.add
+            )
+
+        def finish(g, j):
             nc.vector.scalar_tensor_tensor(
-                out=result_of[g][:, j, :],
+                out=result_tile(g)[:, j, :],
                 in0=a_of[g][:, j, :],
                 scalar=gain_of[g][:, j : j + 1],
                 in1=shifted_of[g][:, j, :],
                 op0=ALU.mult,
                 op1=ALU.add,
             )
-            if j == TILES - 1:
+
+        def store(g, j=None):
+            b, hc, ht = place(g)
+            if j is None:
                 nc.sync.dma_start(out=out_rows[b, :, TILES * ht : TILES * (ht + 1), :], in_=result_of[g][:])
+            else:
+                nc.sync.dma_start(out=out_rows[b, :, TILES * ht + j, :], in_=result_of[g][:, j, :])
 
         def run(stage, g, *args):
             if 0 <= g < GROUPS:
@@ -273,11 +317,20 @@ def tile_swintransformerblock_pb_t_kernel(
             run(load_x, i + X_LOAD_AHEAD)
             for pair in range(TILES // 2):
                 run(transposes, i + TRANSPOSE_AHEAD, pair)
-            run(shift_x, i - 2, 0)
-            run(shift_x, i - 2, 1)
-            helper = shift_x_on_gpsimd if i < GROUPS else shift_x_on_vector
-            run(helper, i - 2, 2)
-            run(helper, i - 2, 3)
+            if i == -TRANSPOSE_AHEAD:
+                spread_bias()
+            beside_bias_adds = i < GROUPS
+            if beside_bias_adds:
+                run(scale_a, i - 2, 3)
+                run(shift_x, i - 2, 0)
+                run(shift_x, i - 2, 1)
+                run(shift_x_on_gpsimd, i - 2, 2)
+                run(add_x_on_gpsimd, i - 2, 3)
+            else:
+                run(shift_x, i - 2, 0)
+                run(shift_x, i - 2, 1)
+                run(shift_x_on_vector, i - 2, 2)
+                run(shift_x_on_vector, i - 2, 3)
             for j in range(TILES):
                 run(add_bias, i, j)
             for j in range(TILES):
@@ -287,8 +340,16 @@ def tile_swintransformerblock_pb_t_kernel(
             run(regroup, i + TRANSPOSE_AHEAD, 0)
             run(root, i)
             run(regroup, i + TRANSPOSE_AHEAD, 1)
-            for j in range(TILES):
-                run(finish, i - 2, j)
+            for j in range(TILES - 1 if beside_bias_adds else TILES):
                 run(chain, i - 1, j)
+                run(finish, i - 2, j)
+                if i - 2 == GROUPS - 1:
+                    run(store, i - 2, j)
+            if i - 2 < GROUPS - 1:
+                run(store, i - 2)
+            if beside_bias_adds:
+                run(chain, i - 1, 3)
             run(quantise, i + QUANTISE_AHEAD)
+            if i == -QUANTISE_AHEAD:
+                scale_constants()
             run(chain, i - 1, 4)

@@ -28,6 +28,7 @@ QUANTISE_AHEAD = 2
 TRANSPOSE_AHEAD = 3
 O_LOAD_AHEAD = 5
 X_LOAD_AHEAD = 3
+SCALAR_COLS = 256
 
 
 def tile_swintransformerblock_pb_t_kernel(
@@ -152,17 +153,18 @@ def tile_swintransformerblock_pb_t_kernel(
                 in_=tp_of[g, pair][:].rearrange("p u n -> p n u"),
             )
 
-        def quantise(g):
-            codes = mx_pool.tile([P, TILES * P], U32, align_bytes=64)
-            scales = mx_pool.tile([P, TILES * P], U8, align_bytes=64)
-            width = TILES * P // 2 if g == 0 else TILES * P
-            for n in range(0, TILES * P, width):
-                nc.vector.quantize_mx(
-                    out=codes[:, n : n + width].bitcast(FP8X4),
-                    scales=scales[:, n : n + width],
-                    in_=grouped_of[g][:, 4 * n : 4 * (n + width)],
-                )
-            codes_of[g], scales_of[g] = codes, scales
+        def quantise(g, half):
+            if half == 0:
+                codes = mx_pool.tile([P, TILES * P], U32, align_bytes=64)
+                scales = mx_pool.tile([P, TILES * P], U8, align_bytes=64)
+                codes_of[g], scales_of[g] = codes, scales
+            width = TILES * P // 2
+            n = width * half
+            nc.vector.quantize_mx(
+                out=codes_of[g][:, n : n + width].bitcast(FP8X4),
+                scales=scales_of[g][:, n : n + width],
+                in_=grouped_of[g][:, 4 * n : 4 * (n + width)],
+            )
 
         def project(g, j):
             y = y_pool.tile([P, C], F32, tag="y")
@@ -247,19 +249,19 @@ def tile_swintransformerblock_pb_t_kernel(
                 shifted_of[g] = shifted
             return shifted_of[g]
 
-        def shift_x(g, j):
+        def shift_x(g, j, cols=slice(0, C)):
             nc.scalar.activation(
-                out=shifted_tile(g)[:, j, :],
-                in_=x_of[g][:, j, :],
+                out=shifted_tile(g)[:, j, cols],
+                in_=x_of[g][:, j, cols],
                 func=ACT.Identity,
                 bias=offset_of[g][:, j : j + 1],
                 scale=1.0,
             )
 
-        def shift_x_on_gpsimd(g, j):
+        def shift_x_on_gpsimd(g, j, cols=slice(0, C)):
             nc.gpsimd.tensor_scalar(
-                out=shifted_of[g][:, j, :],
-                in0=x_of[g][:, j, :],
+                out=shifted_of[g][:, j, cols],
+                in0=x_of[g][:, j, cols],
                 scalar1=1.0,
                 scalar2=offset_of[g][:, j : j + 1],
                 op0=ALU.mult,
@@ -323,14 +325,17 @@ def tile_swintransformerblock_pb_t_kernel(
             if beside_bias_adds:
                 run(scale_a, i - 2, 3)
                 run(shift_x, i - 2, 0)
-                run(shift_x, i - 2, 1)
+                run(shift_x, i - 2, 1, slice(0, SCALAR_COLS))
                 run(shift_x_on_gpsimd, i - 2, 2)
                 run(add_x_on_gpsimd, i - 2, 3)
+                run(shift_x_on_gpsimd, i - 2, 1, slice(SCALAR_COLS, C))
+                vector_tiles = (0, 1, 2)
             else:
                 run(shift_x, i - 2, 0)
                 run(shift_x, i - 2, 1)
                 run(shift_x_on_vector, i - 2, 2)
                 run(shift_x_on_vector, i - 2, 3)
+                vector_tiles = (2, 3, 0, 1)
             for j in range(TILES):
                 run(add_bias, i, j)
             for j in range(TILES):
@@ -340,8 +345,8 @@ def tile_swintransformerblock_pb_t_kernel(
             run(regroup, i + TRANSPOSE_AHEAD, 0)
             run(root, i)
             run(regroup, i + TRANSPOSE_AHEAD, 1)
-            for j in range(TILES - 1 if beside_bias_adds else TILES):
-                run(chain, i - 1, j)
+            for step, j in enumerate(vector_tiles):
+                run(chain, i - 1, step)
                 run(finish, i - 2, j)
                 if i - 2 == GROUPS - 1:
                     run(store, i - 2, j)
@@ -349,7 +354,8 @@ def tile_swintransformerblock_pb_t_kernel(
                 run(store, i - 2)
             if beside_bias_adds:
                 run(chain, i - 1, 3)
-            run(quantise, i + QUANTISE_AHEAD)
+            run(quantise, i + QUANTISE_AHEAD, 0)
+            run(chain, i - 1, 4)
+            run(quantise, i + QUANTISE_AHEAD, 1)
             if i == -QUANTISE_AHEAD:
                 scale_constants()
-            run(chain, i - 1, 4)

@@ -153,18 +153,17 @@ def tile_swintransformerblock_pb_t_kernel(
                 in_=tp_of[g, pair][:].rearrange("p u n -> p n u"),
             )
 
-        def quantise(g, half):
-            if half == 0:
-                codes = mx_pool.tile([P, TILES * P], U32, align_bytes=64)
-                scales = mx_pool.tile([P, TILES * P], U8, align_bytes=64)
-                codes_of[g], scales_of[g] = codes, scales
-            width = TILES * P // 2
-            n = width * half
-            nc.vector.quantize_mx(
-                out=codes_of[g][:, n : n + width].bitcast(FP8X4),
-                scales=scales_of[g][:, n : n + width],
-                in_=grouped_of[g][:, 4 * n : 4 * (n + width)],
-            )
+        def quantise(g):
+            codes = mx_pool.tile([P, TILES * P], U32, align_bytes=64)
+            scales = mx_pool.tile([P, TILES * P], U8, align_bytes=64)
+            width = TILES * P // 2 if g == 0 else TILES * P
+            for n in range(0, TILES * P, width):
+                nc.vector.quantize_mx(
+                    out=codes[:, n : n + width].bitcast(FP8X4),
+                    scales=scales[:, n : n + width],
+                    in_=grouped_of[g][:, 4 * n : 4 * (n + width)],
+                )
+            codes_of[g], scales_of[g] = codes, scales
 
         def project(g, j):
             y = y_pool.tile([P, C], F32, tag="y")
@@ -212,22 +211,25 @@ def tile_swintransformerblock_pb_t_kernel(
             nc.scalar.activation(out=std[:], in_=sumsq_of[g][:], func=ACT.Sqrt, scale=1.0 / (C - 1))
             std_of[g] = std
 
+        def add_eps(g):
+            denom = stats.tile([P, TILES], F32)
+            nc.scalar.activation(out=denom[:], in_=std_of[g][:], func=ACT.Identity, bias=EPS, scale=1.0)
+            denom_of[g] = denom
+
+        CHAIN = 4
+
         def chain(g, step):
             b, hc, ht = place(g)
             tiles_of_image = slice(TILES * ht, TILES * (ht + 1))
             if step == 0:
-                denom = stats.tile([P, TILES], F32)
-                nc.vector.tensor_scalar_add(out=denom[:], in0=std_of[g][:], scalar1=EPS)
-                denom_of[g] = denom
-            elif step == 1:
                 recip = stats.tile([P, TILES], F32)
                 nc.vector.reciprocal(out=recip[:], in_=denom_of[g][:])
                 recip_of[g] = recip
-            elif step == 2:
+            elif step == 1:
                 gain = stats.tile([P, TILES], F32)
                 nc.vector.tensor_mul(out=gain[:], in0=recip_of[g][:], in1=ada_scale_s[:, tiles_of_image])
                 gain_of[g] = gain
-            elif step == 3:
+            elif step == 2:
                 centre = stats.tile([P, TILES], F32)
                 nc.vector.scalar_tensor_tensor(
                     out=centre[:],
@@ -321,21 +323,22 @@ def tile_swintransformerblock_pb_t_kernel(
                 run(transposes, i + TRANSPOSE_AHEAD, pair)
             if i == -TRANSPOSE_AHEAD:
                 spread_bias()
-            beside_bias_adds = i < GROUPS
-            if beside_bias_adds:
+            if i < GROUPS:
                 run(scale_a, i - 2, 3)
                 run(shift_x, i - 2, 0)
                 run(shift_x, i - 2, 1, slice(0, SCALAR_COLS))
                 run(shift_x_on_gpsimd, i - 2, 2)
                 run(add_x_on_gpsimd, i - 2, 3)
                 run(shift_x_on_gpsimd, i - 2, 1, slice(SCALAR_COLS, C))
-                vector_tiles = (0, 1, 2)
+                vector_work = [(finish, 0), (finish, 1), (finish, 2)]
+            elif i == GROUPS:
+                for j in range(TILES - 1):
+                    run(shift_x, i - 2, j)
+                vector_work = [(shift_x_on_vector, 3), (finish, 3), (finish, 0), (finish, 1), (finish, 2)]
             else:
-                run(shift_x, i - 2, 0)
-                run(shift_x, i - 2, 1)
-                run(shift_x_on_vector, i - 2, 2)
-                run(shift_x_on_vector, i - 2, 3)
-                vector_tiles = (2, 3, 0, 1)
+                for j in range(TILES):
+                    run(shift_x, i - 2, j)
+                vector_work = [(finish, 0), (finish, 1), (finish, 2), (finish, 3)]
             for j in range(TILES):
                 run(add_bias, i, j)
             for j in range(TILES):
@@ -345,17 +348,17 @@ def tile_swintransformerblock_pb_t_kernel(
             run(regroup, i + TRANSPOSE_AHEAD, 0)
             run(root, i)
             run(regroup, i + TRANSPOSE_AHEAD, 1)
-            for step, j in enumerate(vector_tiles):
-                run(chain, i - 1, step)
-                run(finish, i - 2, j)
+            run(add_eps, i)
+            for k, (stage, j) in enumerate(vector_work):
+                if k < CHAIN:
+                    run(chain, i - 1, k)
+                run(stage, i - 2, j)
                 if i - 2 == GROUPS - 1:
                     run(store, i - 2, j)
             if i - 2 < GROUPS - 1:
                 run(store, i - 2)
-            if beside_bias_adds:
-                run(chain, i - 1, 3)
-            run(quantise, i + QUANTISE_AHEAD, 0)
-            run(chain, i - 1, 4)
-            run(quantise, i + QUANTISE_AHEAD, 1)
+            for k in range(len(vector_work), CHAIN):
+                run(chain, i - 1, k)
+            run(quantise, i + QUANTISE_AHEAD)
             if i == -QUANTISE_AHEAD:
                 scale_constants()

@@ -43,11 +43,11 @@ def tile_swintransformerblock_pb_t_kernel(
     with ExitStack() as ctx:
         ctx.enter_context(tc.manual_schedule())
         const = ctx.enter_context(tc.tile_pool(name="const", bufs=1))
-        o_pool = ctx.enter_context(tc.tile_pool(name="o", bufs=4))
+        o_pool = ctx.enter_context(tc.tile_pool(name="o", bufs=5))
         x_pool = ctx.enter_context(tc.tile_pool(name="x", bufs=6))
-        mx_pool = ctx.enter_context(tc.tile_pool(name="mx", bufs=3))
-        work = ctx.enter_context(tc.tile_pool(name="work", bufs=3))
-        stats = ctx.enter_context(tc.tile_pool(name="stats", bufs=3))
+        mx_pool = ctx.enter_context(tc.tile_pool(name="mx", bufs=4))
+        work = ctx.enter_context(tc.tile_pool(name="work", bufs=5))
+        stats = ctx.enter_context(tc.tile_pool(name="stats", bufs=5))
         tp_pool = ctx.enter_context(tc.psum_pool(name="tp", bufs=4))
         y_pool = ctx.enter_context(tc.psum_pool(name="y", bufs=4))
 
@@ -325,13 +325,15 @@ def tile_swintransformerblock_pb_t_kernel(
                 spread_bias()
             if i < GROUPS:
                 run(scale_a, i - 2, 3)
-                run(shift_x, i - 2, 0)
                 run(shift_x, i - 2, 1, slice(0, SCALAR_COLS))
+                run(shift_x, i - 2, 0)
+                run(add_eps, i - 1)
                 run(shift_x_on_gpsimd, i - 2, 2)
                 run(add_x_on_gpsimd, i - 2, 3)
                 run(shift_x_on_gpsimd, i - 2, 1, slice(SCALAR_COLS, C))
                 vector_work = [(finish, 0), (finish, 1), (finish, 2)]
             elif i == GROUPS:
+                run(add_eps, i - 1)
                 for j in range(TILES - 1):
                     run(shift_x, i - 2, j)
                 vector_work = [(shift_x_on_vector, 3), (finish, 3), (finish, 0), (finish, 1), (finish, 2)]
@@ -348,7 +350,6 @@ def tile_swintransformerblock_pb_t_kernel(
             run(regroup, i + TRANSPOSE_AHEAD, 0)
             run(root, i)
             run(regroup, i + TRANSPOSE_AHEAD, 1)
-            run(add_eps, i)
             for k, (stage, j) in enumerate(vector_work):
                 if k < CHAIN:
                     run(chain, i - 1, k)

@@ -59,16 +59,15 @@ def tile_swintransformerblock_pb_t_kernel(
             b, hc = divmod(g, 2)
             return b, hc, 1 - hc
 
-        def load_o(g):
+        def load_o(g, first=0, count=TILES):
             b, hc, ht = place(g)
-            o_sb = o_pool.tile([P, TILES, C], BF16)
-            step = TILES // 2 if g == 0 else TILES
-            for j in range(0, TILES, step):
-                nc.sync.dma_start(
-                    out=o_sb[:, j : j + step, :],
-                    in_=o_rows[P * b : P * (b + 1), TILES * hc + j : TILES * hc + j + step, :],
-                )
-            o_of[g] = o_sb
+            if g not in o_of:
+                o_sb = o_pool.tile([P, TILES, C], BF16)
+                o_of[g] = o_sb
+            nc.sync.dma_start(
+                out=o_of[g][:, first : first + count, :],
+                in_=o_rows[P * b : P * (b + 1), TILES * hc + first : TILES * hc + first + count, :],
+            )
 
         def load_x(g):
             b, hc, ht = place(g)
@@ -76,17 +75,18 @@ def tile_swintransformerblock_pb_t_kernel(
             nc.sync.dma_start(out=x_sb[:], in_=x_rows[b, :, TILES * ht : TILES * (ht + 1), :])
             x_of[g] = x_sb
 
-        load_o(0)
+        load_o(0, 0, TILES // 2)
 
         w_words = const.tile([P, 2 * C], U8, align_bytes=64)
         w_scales = const.tile([P, C], U8, align_bytes=64)
         nc.vector.memset(w_scales[:].bitcast(I32), 0)
-        nc.sync.dma_start(out=w_words[:].bitcast(I32), in_=out_w_words[0].bitcast(I32))
         for quadrant in range(4):
             nc.sync.dma_start(
                 out=w_scales[32 * quadrant : 32 * quadrant + 4, :].bitcast(I32),
                 in_=out_w_scales[0, 4 * quadrant : 4 * quadrant + 4, :].bitcast(I32),
             )
+        nc.sync.dma_start(out=w_words[:].bitcast(I32), in_=out_w_words[0].bitcast(I32))
+        load_o(0, TILES // 2, TILES // 2)
         for g in range(1, O_LOAD_AHEAD - TRANSPOSE_AHEAD):
             load_o(g)
 
@@ -99,6 +99,9 @@ def tile_swintransformerblock_pb_t_kernel(
         nc.scalar.dma_start(out=ada_scale_sb[:], in_=ada1_scale[0].rearrange("(m t) u -> m (t u)", t=RUN))
         ada_shift_sb = const.tile([P, RUN], BF16)
         nc.scalar.dma_start(out=ada_shift_sb[:], in_=ada1_shift[0].rearrange("(m t) u -> m (t u)", t=RUN))
+        warm = const.tile([P, 2], F32)
+        nc.vector.memset(warm[:, 0:1], 1.0)
+        nc.scalar.activation(out=warm[:, 1:2], in_=warm[:, 0:1], func=ACT.Sqrt)
 
         ident = const.tile([P, P], F32)
         make_identity(nc, ident[:])

@@ -28,7 +28,6 @@ QUANTISE_AHEAD = 2
 TRANSPOSE_AHEAD = 3
 O_LOAD_AHEAD = 5
 X_LOAD_AHEAD = 3
-SCALAR_COLS = 256
 
 
 def tile_swintransformerblock_pb_t_kernel(
@@ -48,12 +47,13 @@ def tile_swintransformerblock_pb_t_kernel(
         mx_pool = ctx.enter_context(tc.tile_pool(name="mx", bufs=4))
         work = ctx.enter_context(tc.tile_pool(name="work", bufs=5))
         stats = ctx.enter_context(tc.tile_pool(name="stats", bufs=5))
-        tp_pool = ctx.enter_context(tc.psum_pool(name="tp", bufs=4))
+        tp_pool = ctx.enter_context(tc.psum_pool(name="tp", bufs=2))
+        xp_pool = ctx.enter_context(tc.psum_pool(name="xp", bufs=2))
         y_pool = ctx.enter_context(tc.psum_pool(name="y", bufs=4))
 
         o_of, x_of, grouped_of, codes_of, scales_of, y_of = {}, {}, {}, {}, {}, {}
         a_of, negmean_of, sumsq_of, std_of, gain_of, offset_of, shifted_of = {}, {}, {}, {}, {}, {}, {}
-        tp_of, denom_of, recip_of, centre_of, result_of = {}, {}, {}, {}, {}
+        tp_of, denom_of, recip_of, centre_of, result_of, xp_of = {}, {}, {}, {}, {}, {}
 
         def place(g):
             b, hc = divmod(g, 2)
@@ -119,6 +119,8 @@ def tile_swintransformerblock_pb_t_kernel(
         nc.vector.tensor_copy(out=hi_ij[:, :, 1:4], in_=lo_ij[:, :, 0:3])
         nc.vector.tensor_copy(out=hi_ij[:, :, 0:1], in_=lo_ij[:, :, 3:4])
         perm = [perm_lo, perm_hi]
+        ident_bf = const.tile([P, P], BF16)
+        nc.vector.tensor_copy(out=ident_bf[:], in_=ident[:])
 
         squares = const.tile([P, TILES, C], BF16)
 
@@ -156,17 +158,17 @@ def tile_swintransformerblock_pb_t_kernel(
                 in_=tp_of[g, pair][:].rearrange("p u n -> p n u"),
             )
 
-        def quantise(g):
-            codes = mx_pool.tile([P, TILES * P], U32, align_bytes=64)
-            scales = mx_pool.tile([P, TILES * P], U8, align_bytes=64)
-            width = TILES * P // 2 if g == 0 else TILES * P
-            for n in range(0, TILES * P, width):
-                nc.vector.quantize_mx(
-                    out=codes[:, n : n + width].bitcast(FP8X4),
-                    scales=scales[:, n : n + width],
-                    in_=grouped_of[g][:, 4 * n : 4 * (n + width)],
-                )
-            codes_of[g], scales_of[g] = codes, scales
+        def quantise(g, pair):
+            if pair == 0:
+                codes = mx_pool.tile([P, TILES * P], U32, align_bytes=64)
+                scales = mx_pool.tile([P, TILES * P], U8, align_bytes=64)
+                codes_of[g], scales_of[g] = codes, scales
+            cols = slice(2 * P * pair, 2 * P * (pair + 1))
+            nc.vector.quantize_mx(
+                out=codes_of[g][:, cols].bitcast(FP8X4),
+                scales=scales_of[g][:, cols],
+                in_=grouped_of[g][:, 8 * P * pair : 8 * P * (pair + 1)],
+            )
 
         def project(g, j):
             y = y_pool.tile([P, C], F32, tag="y")
@@ -254,19 +256,19 @@ def tile_swintransformerblock_pb_t_kernel(
                 shifted_of[g] = shifted
             return shifted_of[g]
 
-        def shift_x(g, j, cols=slice(0, C)):
+        def shift_x(g, j):
             nc.scalar.activation(
-                out=shifted_tile(g)[:, j, cols],
-                in_=x_of[g][:, j, cols],
+                out=shifted_tile(g)[:, j, :],
+                in_=x_of[g][:, j, :],
                 func=ACT.Identity,
                 bias=offset_of[g][:, j : j + 1],
                 scale=1.0,
             )
 
-        def shift_x_on_gpsimd(g, j, cols=slice(0, C)):
+        def shift_x_on_gpsimd(g, j):
             nc.gpsimd.tensor_scalar(
-                out=shifted_of[g][:, j, cols],
-                in0=x_of[g][:, j, cols],
+                out=shifted_tile(g)[:, j, :],
+                in0=x_of[g][:, j, :],
                 scalar1=1.0,
                 scalar2=offset_of[g][:, j : j + 1],
                 op0=ALU.mult,
@@ -292,6 +294,24 @@ def tile_swintransformerblock_pb_t_kernel(
                 bias=offset_of[g][:, j : j + 1],
                 scale=gain_of[g][:, j : j + 1],
             )
+
+        def scale_a_on_gpsimd(g, j):
+            nc.gpsimd.tensor_scalar(
+                out=shifted_tile(g)[:, j, :],
+                in0=a_of[g][:, j, :],
+                scalar1=gain_of[g][:, j : j + 1],
+                scalar2=offset_of[g][:, j : j + 1],
+                op0=ALU.mult,
+                op1=ALU.add,
+            )
+
+        def lay_x(g, j):
+            xp = xp_pool.tile([P, C], F32)
+            nc.tensor.matmul(out=xp[:], lhsT=ident_bf[:], rhs=x_of[g][:, j, :], start=True, stop=True)
+            xp_of[g, j] = xp
+
+        def add_x_from_psum(g, j):
+            nc.vector.tensor_add(out=result_tile(g)[:, j, :], in0=xp_of[g, j][:], in1=shifted_of[g][:, j, :])
 
         def add_x_on_gpsimd(g, j):
             nc.gpsimd.tensor_tensor(
@@ -322,19 +342,26 @@ def tile_swintransformerblock_pb_t_kernel(
         for i in range(-TRANSPOSE_AHEAD, GROUPS + 2):
             run(load_o, i + O_LOAD_AHEAD)
             run(load_x, i + X_LOAD_AHEAD)
+            steady = i < GROUPS
+            through_psum = [j for j in range(2) if j == 0 or i % 2 == 0] if steady else []
             for pair in range(TILES // 2):
                 run(transposes, i + TRANSPOSE_AHEAD, pair)
+            for j in through_psum:
+                run(lay_x, i - 2, j)
             if i == -TRANSPOSE_AHEAD:
                 spread_bias()
-            if i < GROUPS:
-                run(scale_a, i - 2, 3)
-                run(shift_x, i - 2, 1, slice(0, SCALAR_COLS))
-                run(shift_x, i - 2, 0)
+            run(regroup, i + TRANSPOSE_AHEAD, 0)
+            if i < 0:
+                run(regroup, i + TRANSPOSE_AHEAD, 1)
+            if steady:
                 run(add_eps, i - 1)
-                run(shift_x_on_gpsimd, i - 2, 2)
+                run(scale_a, i - 2, 2)
+                run(scale_a, i - 2, 3)
+                for j in range(2):
+                    run(scale_a_on_gpsimd if j in through_psum else shift_x_on_gpsimd, i - 2, j)
+                run(add_x_on_gpsimd, i - 2, 2)
                 run(add_x_on_gpsimd, i - 2, 3)
-                run(shift_x_on_gpsimd, i - 2, 1, slice(SCALAR_COLS, C))
-                vector_work = [(finish, 0), (finish, 1), (finish, 2)]
+                vector_work = [(add_x_from_psum if j in through_psum else finish, j) for j in range(2)]
             elif i == GROUPS:
                 run(add_eps, i - 1)
                 for j in range(TILES - 1):
@@ -350,19 +377,25 @@ def tile_swintransformerblock_pb_t_kernel(
                 run(project, i + MATMUL_AHEAD, j)
             for j in range(TILES):
                 run(square, i, j)
-            run(regroup, i + TRANSPOSE_AHEAD, 0)
+            if i >= 0:
+                run(regroup, i + TRANSPOSE_AHEAD, 1)
             run(root, i)
-            run(regroup, i + TRANSPOSE_AHEAD, 1)
+            step = 0
             for k, (stage, j) in enumerate(vector_work):
-                if k < CHAIN:
-                    run(chain, i - 1, k)
+                if k > 0 or not steady:
+                    if step < CHAIN:
+                        run(chain, i - 1, step)
+                        step += 1
                 run(stage, i - 2, j)
                 if i - 2 == GROUPS - 1:
                     run(store, i - 2, j)
             if i - 2 < GROUPS - 1:
                 run(store, i - 2)
-            for k in range(len(vector_work), CHAIN):
-                run(chain, i - 1, k)
-            run(quantise, i + QUANTISE_AHEAD)
+            if steady:
+                run(chain, i - 1, 1)
+                run(quantise, i + QUANTISE_AHEAD, 0)
+                run(chain, i - 1, 2)
+                run(quantise, i + QUANTISE_AHEAD, 1)
+                run(chain, i - 1, 3)
             if i == -QUANTISE_AHEAD:
                 scale_constants()

@@ -23,11 +23,10 @@ EPS = 1e-5
 
 FLOPS = 2 * IMAGES * 1024 * C * C
 
-MATMUL_AHEAD = 1
-QUANTISE_AHEAD = 2
-TRANSPOSE_AHEAD = 3
-O_LOAD_AHEAD = 5
-X_LOAD_AHEAD = 3
+QUANTISE_AHEAD = 1
+TRANSPOSE_AHEAD = 2
+O_LOAD_AHEAD = 4
+X_LOAD_AHEAD = 2
 
 
 def tile_swintransformerblock_pb_t_kernel(
@@ -53,6 +52,7 @@ def tile_swintransformerblock_pb_t_kernel(
 
         o_of, x_of, grouped_of, codes_of, scales_of, y_of = {}, {}, {}, {}, {}, {}
         a_of, negmean_of, sumsq_of, std_of, gain_of, offset_of, shifted_of = {}, {}, {}, {}, {}, {}, {}
+        scaled_mean_of = {}
         tp_of, denom_of, recip_of, centre_of, result_of, xp_of = {}, {}, {}, {}, {}, {}
 
         def place(g):
@@ -221,29 +221,33 @@ def tile_swintransformerblock_pb_t_kernel(
             nc.scalar.activation(out=denom[:], in_=std_of[g][:], func=ACT.Identity, bias=EPS, scale=1.0)
             denom_of[g] = denom
 
-        CHAIN = 4
+        CHAIN = 5
 
         def chain(g, step):
             b, hc, ht = place(g)
             tiles_of_image = slice(TILES * ht, TILES * (ht + 1))
             if step == 0:
-                recip = stats.tile([P, TILES], F32)
-                nc.vector.reciprocal(out=recip[:], in_=denom_of[g][:])
-                recip_of[g] = recip
-            elif step == 1:
-                gain = stats.tile([P, TILES], F32)
-                nc.vector.tensor_mul(out=gain[:], in0=recip_of[g][:], in1=ada_scale_s[:, tiles_of_image])
-                gain_of[g] = gain
-            elif step == 2:
-                centre = stats.tile([P, TILES], F32)
+                scaled_mean = stats.tile([P, TILES], F32)
                 nc.vector.scalar_tensor_tensor(
-                    out=centre[:],
+                    out=scaled_mean[:],
                     in0=negmean_of[g][:],
                     scalar=-1.0 / C,
-                    in1=gain_of[g][:],
+                    in1=ada_scale_s[:, tiles_of_image],
                     op0=ALU.mult,
                     op1=ALU.mult,
                 )
+                scaled_mean_of[g] = scaled_mean
+            elif step == 1:
+                recip = stats.tile([P, TILES], F32)
+                nc.vector.reciprocal(out=recip[:], in_=denom_of[g][:])
+                recip_of[g] = recip
+            elif step == 2:
+                gain = stats.tile([P, TILES], F32)
+                nc.vector.tensor_mul(out=gain[:], in0=recip_of[g][:], in1=ada_scale_s[:, tiles_of_image])
+                gain_of[g] = gain
+            elif step == 3:
+                centre = stats.tile([P, TILES], F32)
+                nc.vector.tensor_mul(out=centre[:], in0=recip_of[g][:], in1=scaled_mean_of[g][:])
                 centre_of[g] = centre
             else:
                 offset = stats.tile([P, TILES], F32)
@@ -277,7 +281,7 @@ def tile_swintransformerblock_pb_t_kernel(
 
         def shift_x_on_vector(g, j):
             nc.vector.tensor_scalar_add(
-                out=shifted_of[g][:, j, :], in0=x_of[g][:, j, :], scalar1=offset_of[g][:, j : j + 1]
+                out=shifted_tile(g)[:, j, :], in0=x_of[g][:, j, :], scalar1=offset_of[g][:, j : j + 1]
             )
 
         def result_tile(g):
@@ -339,63 +343,110 @@ def tile_swintransformerblock_pb_t_kernel(
             if 0 <= g < GROUPS:
                 stage(g, *args)
 
+        def roles(g):
+            if g == GROUPS - 3:
+                return ["psum", "psum", "gpsimd", "scalar"]
+            if g > GROUPS - 3:
+                return ["vector", "scalar", "scalar", "scalar"]
+            return ["psum", "psum", "gpsimd", "scalar"] if g % 2 == 0 else ["psum", "shift", "gpsimd", "gpsimd"]
+
+        pending = []
+        left = {}
+
+        def tile_done(g, j):
+            if g == GROUPS - 1:
+                store(g, j)
+                return
+            left[g] -= 1
+            if left[g] == 0:
+                store(g)
+
         for i in range(-TRANSPOSE_AHEAD, GROUPS + 2):
             run(load_o, i + O_LOAD_AHEAD)
             run(load_x, i + X_LOAD_AHEAD)
-            steady = i < GROUPS
-            through_psum = [j for j in range(2) if j == 0 or i % 2 == 0] if steady else []
-            for pair in range(TILES // 2):
-                run(transposes, i + TRANSPOSE_AHEAD, pair)
-            for j in through_psum:
-                run(lay_x, i - 2, j)
+            g = i - 2
+            role = roles(g) if g >= 0 else []
+            by = {r: [j for j in range(len(role)) if role[j] == r] for r in ("psum", "shift", "scalar", "gpsimd", "vector")}
+            left[g] = TILES
+            if i == -TRANSPOSE_AHEAD:
+                run(transposes, i + TRANSPOSE_AHEAD, 0)
+            run(transposes, i + TRANSPOSE_AHEAD, 1)
+            for j in by["psum"]:
+                lay_x(g, j)
             if i == -TRANSPOSE_AHEAD:
                 spread_bias()
             run(regroup, i + TRANSPOSE_AHEAD, 0)
             if i < 0:
                 run(regroup, i + TRANSPOSE_AHEAD, 1)
-            if steady:
-                run(add_eps, i - 1)
-                run(scale_a, i - 2, 2)
-                run(scale_a, i - 2, 3)
-                for j in range(2):
-                    run(scale_a_on_gpsimd if j in through_psum else shift_x_on_gpsimd, i - 2, j)
-                run(add_x_on_gpsimd, i - 2, 2)
-                run(add_x_on_gpsimd, i - 2, 3)
-                vector_work = [(add_x_from_psum if j in through_psum else finish, j) for j in range(2)]
-            elif i == GROUPS:
-                run(add_eps, i - 1)
-                for j in range(TILES - 1):
-                    run(shift_x, i - 2, j)
-                vector_work = [(shift_x_on_vector, 3), (finish, 3), (finish, 0), (finish, 1), (finish, 2)]
             else:
-                for j in range(TILES):
-                    run(shift_x, i - 2, j)
-                vector_work = [(finish, 0), (finish, 1), (finish, 2), (finish, 3)]
+                run(transposes, i + TRANSPOSE_AHEAD + 1, 0)
+            run(add_eps, i - 1)
+            late = g >= GROUPS - 3
+            if late:
+                for j in by["gpsimd"]:
+                    scale_a(g, j)
+                for j in by["scalar"]:
+                    shift_x(g, j)
+            for j in by["psum"]:
+                scale_a_on_gpsimd(g, j)
+            for j in by["shift"]:
+                shift_x_on_gpsimd(g, j)
+            if late:
+                pending += [(g, j) for j in by["gpsimd"]]
+            n = len(pending) if late else 2 if g % 2 == 0 else 1
+            for k, j in pending[:n]:
+                add_x_on_gpsimd(k, j)
+                tile_done(k, j)
+            pending = pending[n:]
+            if not late:
+                pending += [(g, j) for j in by["gpsimd"]]
+            def quantise_next():
+                run(quantise, i + QUANTISE_AHEAD, 0)
+                run(quantise, i + QUANTISE_AHEAD, 1)
+                if i == -QUANTISE_AHEAD:
+                    scale_constants()
             for j in range(TILES):
                 run(add_bias, i, j)
-            for j in range(TILES):
-                run(project, i + MATMUL_AHEAD, j)
+                if i in (0, 1) and j == 1:
+                    quantise_next()
+            if i < 0:
+                quantise_next()
             for j in range(TILES):
                 run(square, i, j)
+                if j == 1 and not late:
+                    for t in by["scalar"]:
+                        shift_x(g, t)
+            if not late:
+                for t in by["gpsimd"]:
+                    scale_a(g, t)
             if i >= 0:
                 run(regroup, i + TRANSPOSE_AHEAD, 1)
             run(root, i)
-            step = 0
-            for k, (stage, j) in enumerate(vector_work):
-                if k > 0 or not steady:
-                    if step < CHAIN:
-                        run(chain, i - 1, step)
-                        step += 1
-                run(stage, i - 2, j)
-                if i - 2 == GROUPS - 1:
-                    run(store, i - 2, j)
-            if i - 2 < GROUPS - 1:
-                run(store, i - 2)
-            if steady:
-                run(chain, i - 1, 1)
+            def last_pass(stage, j):
+                stage(g, j)
+                tile_done(g, j)
+            for j in by["vector"]:
+                shift_x_on_vector(g, j)
+            for j in by["psum"]:
+                last_pass(add_x_from_psum, j)
+            run(chain, i - 1, 0)
+            run(chain, i - 1, 1)
+            if i > 1:
                 run(quantise, i + QUANTISE_AHEAD, 0)
-                run(chain, i - 1, 2)
+            from_sbuf = by["vector"] + by["scalar"] + by["shift"]
+            early = 1 if len(from_sbuf) > 1 else 0
+            for j in from_sbuf[:early]:
+                last_pass(finish, j)
+            run(chain, i - 1, 2)
+            run(chain, i - 1, 3)
+            for j in from_sbuf[early : early + 1]:
+                last_pass(finish, j)
+            run(chain, i - 1, 4)
+            for j in from_sbuf[early + 1 :]:
+                last_pass(finish, j)
+            if i > 1:
                 run(quantise, i + QUANTISE_AHEAD, 1)
-                run(chain, i - 1, 3)
-            if i == -QUANTISE_AHEAD:
-                scale_constants()
+            for t in range(TILES):
+                run(project, i + QUANTISE_AHEAD, t)
+            if i < 0:
+                run(transposes, i + TRANSPOSE_AHEAD + 1, 0)

@@ -23,9 +23,9 @@ EPS = 1e-5
 
 FLOPS = 2 * IMAGES * 1024 * C * C
 
-QUANTISE_AHEAD = 1
-TRANSPOSE_AHEAD = 2
-O_LOAD_AHEAD = 4
+QUANTISE_AHEAD = 2
+COPY_AHEAD = 2
+O_LOAD_AHEAD = 5
 X_LOAD_AHEAD = 2
 
 
@@ -87,14 +87,14 @@ def tile_swintransformerblock_pb_t_kernel(
             )
         nc.sync.dma_start(out=w_words[:].bitcast(I32), in_=out_w_words[0].bitcast(I32))
         load_o(0, TILES // 2, TILES // 2)
-        for g in range(1, O_LOAD_AHEAD - TRANSPOSE_AHEAD):
+        for g in range(1, 3):
             load_o(g)
 
         bias_row = const.tile([P, C], BF16)
         nc.vector.memset(bias_row[:], 0.0)
         nc.scalar.dma_start(out=bias_row[0:1, :], in_=out_b.rearrange("(u c) -> u c", u=1))
         ones = const.tile([P, P], BF16)
-        nc.vector.memset(ones[:], 1.0)
+        nc.vector.memset(ones[:], -1.0 / C)
         ada_scale_sb = const.tile([P, RUN], BF16)
         nc.scalar.dma_start(out=ada_scale_sb[:], in_=ada1_scale[0].rearrange("(m t) u -> m (t u)", t=RUN))
         ada_shift_sb = const.tile([P, RUN], BF16)
@@ -132,8 +132,10 @@ def tile_swintransformerblock_pb_t_kernel(
             nc.tensor.matmul(out=bias_ps[:], lhsT=ones[:], rhs=bias_row[:], start=True, stop=True)
 
         def scale_constants():
-            nc.vector.tensor_scalar_mul(out=bias_s[:], in0=bias_ps[:], scalar1=-1.0 / C)
-            nc.vector.tensor_scalar_mul(out=ada_scale_s[:], in0=ada_scale_sb[:], scalar1=-1.0 * C)
+            nc.scalar.copy(out=bias_s[:], in_=bias_ps[:])
+            nc.gpsimd.tensor_scalar(
+                out=ada_scale_s[:], in0=ada_scale_sb[:], scalar1=-1.0 * C, scalar2=0.0, op0=ALU.mult, op1=ALU.add
+            )
 
         def transposes(g, pair):
             b, hc, ht = place(g)
@@ -361,27 +363,40 @@ def tile_swintransformerblock_pb_t_kernel(
             if left[g] == 0:
                 store(g)
 
-        for i in range(-TRANSPOSE_AHEAD, GROUPS + 2):
+        for pair in range(TILES // 2):
+            transposes(0, pair)
+            regroup(0, pair)
+        spread_bias()
+        scale_constants()
+        load_o(3)
+        load_x(0)
+        quantise(0, 0)
+        quantise(0, 1)
+        for pair in range(TILES // 2):
+            transposes(1, pair)
+            regroup(1, pair)
+        for j in range(TILES):
+            project(0, j)
+        load_o(4)
+        load_x(1)
+        transposes(2, 0)
+        transposes(2, 1)
+
+        for i in range(GROUPS + 2):
             run(load_o, i + O_LOAD_AHEAD)
             run(load_x, i + X_LOAD_AHEAD)
             g = i - 2
             role = roles(g) if g >= 0 else []
             by = {r: [j for j in range(len(role)) if role[j] == r] for r in ("psum", "shift", "scalar", "gpsimd", "vector")}
             left[g] = TILES
-            if i == -TRANSPOSE_AHEAD:
-                run(transposes, i + TRANSPOSE_AHEAD, 0)
-            run(transposes, i + TRANSPOSE_AHEAD, 1)
-            for j in by["psum"]:
-                lay_x(g, j)
-            if i == -TRANSPOSE_AHEAD:
-                spread_bias()
-            run(regroup, i + TRANSPOSE_AHEAD, 0)
-            if i < 0:
-                run(regroup, i + TRANSPOSE_AHEAD, 1)
-            else:
-                run(transposes, i + TRANSPOSE_AHEAD + 1, 0)
-            run(add_eps, i - 1)
             late = g >= GROUPS - 3
+
+            def last_pass(stage, j):
+                stage(g, j)
+                tile_done(g, j)
+
+            run(regroup, i + COPY_AHEAD, 0)
+            run(add_eps, i - 1)
             if late:
                 for j in by["gpsimd"]:
                     scale_a(g, j)
@@ -400,39 +415,37 @@ def tile_swintransformerblock_pb_t_kernel(
             pending = pending[n:]
             if not late:
                 pending += [(g, j) for j in by["gpsimd"]]
-            def quantise_next():
-                run(quantise, i + QUANTISE_AHEAD, 0)
-                run(quantise, i + QUANTISE_AHEAD, 1)
-                if i == -QUANTISE_AHEAD:
-                    scale_constants()
             for j in range(TILES):
                 run(add_bias, i, j)
-                if i in (0, 1) and j == 1:
-                    quantise_next()
-            if i < 0:
-                quantise_next()
+                if i == 0 and j == 1:
+                    quantise(1, 0)
+                    quantise(1, 1)
             for j in range(TILES):
+                run(project, i + 1, j)
+                if j == TILES - 1:
+                    run(transposes, i + COPY_AHEAD + 1, 0)
                 run(square, i, j)
-                if j == 1 and not late:
-                    for t in by["scalar"]:
-                        shift_x(g, t)
+                if j == 1:
+                    run(regroup, i + COPY_AHEAD, 1)
+                    if not late:
+                        for t in by["scalar"]:
+                            shift_x(g, t)
+            run(transposes, i + COPY_AHEAD + 1, 1)
             if not late:
                 for t in by["gpsimd"]:
                     scale_a(g, t)
-            if i >= 0:
-                run(regroup, i + TRANSPOSE_AHEAD, 1)
             run(root, i)
-            def last_pass(stage, j):
-                stage(g, j)
-                tile_done(g, j)
             for j in by["vector"]:
                 shift_x_on_vector(g, j)
             for j in by["psum"]:
                 last_pass(add_x_from_psum, j)
+            if 0 <= g + 1 < GROUPS - 2:
+                for j in range(TILES):
+                    if roles(g + 1)[j] == "psum":
+                        lay_x(g + 1, j)
             run(chain, i - 1, 0)
             run(chain, i - 1, 1)
-            if i > 1:
-                run(quantise, i + QUANTISE_AHEAD, 0)
+            run(quantise, i + QUANTISE_AHEAD, 0)
             from_sbuf = by["vector"] + by["scalar"] + by["shift"]
             early = 1 if len(from_sbuf) > 1 else 0
             for j in from_sbuf[:early]:
@@ -444,9 +457,4 @@ def tile_swintransformerblock_pb_t_kernel(
             run(chain, i - 1, 4)
             for j in from_sbuf[early + 1 :]:
                 last_pass(finish, j)
-            if i > 1:
-                run(quantise, i + QUANTISE_AHEAD, 1)
-            for t in range(TILES):
-                run(project, i + QUANTISE_AHEAD, t)
-            if i < 0:
-                run(transposes, i + TRANSPOSE_AHEAD + 1, 0)
+            run(quantise, i + QUANTISE_AHEAD, 1)

@@ -26,7 +26,8 @@ FLOPS = 2 * IMAGES * 1024 * C * C
 QUANTISE_AHEAD = 2
 COPY_AHEAD = 2
 O_LOAD_AHEAD = 5
-X_LOAD_AHEAD = 2
+X_LOAD_AHEAD = 1
+PSUM_COLS = 704
 
 
 def tile_swintransformerblock_pb_t_kernel(
@@ -42,7 +43,7 @@ def tile_swintransformerblock_pb_t_kernel(
         ctx.enter_context(tc.manual_schedule())
         const = ctx.enter_context(tc.tile_pool(name="const", bufs=1))
         o_pool = ctx.enter_context(tc.tile_pool(name="o", bufs=5))
-        x_pool = ctx.enter_context(tc.tile_pool(name="x", bufs=6))
+        x_pool = ctx.enter_context(tc.tile_pool(name="x", bufs=7))
         mx_pool = ctx.enter_context(tc.tile_pool(name="mx", bufs=4))
         work = ctx.enter_context(tc.tile_pool(name="work", bufs=5))
         stats = ctx.enter_context(tc.tile_pool(name="stats", bufs=5))
@@ -51,8 +52,7 @@ def tile_swintransformerblock_pb_t_kernel(
         y_pool = ctx.enter_context(tc.psum_pool(name="y", bufs=4))
 
         o_of, x_of, grouped_of, codes_of, scales_of, y_of = {}, {}, {}, {}, {}, {}
-        a_of, negmean_of, sumsq_of, std_of, gain_of, offset_of, shifted_of = {}, {}, {}, {}, {}, {}, {}
-        scaled_mean_of = {}
+        a_of, negmean_of, sumsq_of, std_of, gain_of, offset_of = {}, {}, {}, {}, {}, {}
         tp_of, denom_of, recip_of, centre_of, result_of, xp_of = {}, {}, {}, {}, {}, {}
 
         def place(g):
@@ -223,68 +223,32 @@ def tile_swintransformerblock_pb_t_kernel(
             nc.scalar.activation(out=denom[:], in_=std_of[g][:], func=ACT.Identity, bias=EPS, scale=1.0)
             denom_of[g] = denom
 
-        CHAIN = 5
-
         def chain(g, step):
             b, hc, ht = place(g)
             tiles_of_image = slice(TILES * ht, TILES * (ht + 1))
             if step == 0:
-                scaled_mean = stats.tile([P, TILES], F32)
-                nc.vector.scalar_tensor_tensor(
-                    out=scaled_mean[:],
-                    in0=negmean_of[g][:],
-                    scalar=-1.0 / C,
-                    in1=ada_scale_s[:, tiles_of_image],
-                    op0=ALU.mult,
-                    op1=ALU.mult,
-                )
-                scaled_mean_of[g] = scaled_mean
-            elif step == 1:
                 recip = stats.tile([P, TILES], F32)
                 nc.vector.reciprocal(out=recip[:], in_=denom_of[g][:])
                 recip_of[g] = recip
-            elif step == 2:
+            elif step == 1:
                 gain = stats.tile([P, TILES], F32)
                 nc.vector.tensor_mul(out=gain[:], in0=recip_of[g][:], in1=ada_scale_s[:, tiles_of_image])
                 gain_of[g] = gain
-            elif step == 3:
+            elif step == 2:
                 centre = stats.tile([P, TILES], F32)
-                nc.vector.tensor_mul(out=centre[:], in0=recip_of[g][:], in1=scaled_mean_of[g][:])
+                nc.vector.scalar_tensor_tensor(
+                    out=centre[:],
+                    in0=negmean_of[g][:],
+                    scalar=-1.0 / C,
+                    in1=gain_of[g][:],
+                    op0=ALU.mult,
+                    op1=ALU.mult,
+                )
                 centre_of[g] = centre
             else:
                 offset = stats.tile([P, TILES], F32)
                 nc.vector.tensor_add(out=offset[:], in0=centre_of[g][:], in1=ada_shift_sb[:, tiles_of_image])
                 offset_of[g] = offset
-
-        def shifted_tile(g):
-            if g not in shifted_of:
-                shifted = work.tile([P, TILES, C], F32)
-                shifted_of[g] = shifted
-            return shifted_of[g]
-
-        def shift_x(g, j):
-            nc.scalar.activation(
-                out=shifted_tile(g)[:, j, :],
-                in_=x_of[g][:, j, :],
-                func=ACT.Identity,
-                bias=offset_of[g][:, j : j + 1],
-                scale=1.0,
-            )
-
-        def shift_x_on_gpsimd(g, j):
-            nc.gpsimd.tensor_scalar(
-                out=shifted_tile(g)[:, j, :],
-                in0=x_of[g][:, j, :],
-                scalar1=1.0,
-                scalar2=offset_of[g][:, j : j + 1],
-                op0=ALU.mult,
-                op1=ALU.add,
-            )
-
-        def shift_x_on_vector(g, j):
-            nc.vector.tensor_scalar_add(
-                out=shifted_tile(g)[:, j, :], in0=x_of[g][:, j, :], scalar1=offset_of[g][:, j : j + 1]
-            )
 
         def result_tile(g):
             if g not in result_of:
@@ -292,18 +256,18 @@ def tile_swintransformerblock_pb_t_kernel(
                 result_of[g] = result
             return result_of[g]
 
-        def scale_a(g, j):
+        def scale_on_scalar(g, j):
             nc.scalar.activation(
-                out=shifted_tile(g)[:, j, :],
+                out=result_tile(g)[:, j, :],
                 in_=a_of[g][:, j, :],
                 func=ACT.Identity,
                 bias=offset_of[g][:, j : j + 1],
                 scale=gain_of[g][:, j : j + 1],
             )
 
-        def scale_a_on_gpsimd(g, j):
-            nc.gpsimd.tensor_scalar(
-                out=shifted_tile(g)[:, j, :],
+        def scale_on_vector(g, j):
+            nc.vector.tensor_scalar(
+                out=result_tile(g)[:, j, :],
                 in0=a_of[g][:, j, :],
                 scalar1=gain_of[g][:, j : j + 1],
                 scalar2=offset_of[g][:, j : j + 1],
@@ -311,25 +275,40 @@ def tile_swintransformerblock_pb_t_kernel(
                 op1=ALU.add,
             )
 
-        def lay_x(g, j):
+        def lay_x(g, j, cols):
             xp = xp_pool.tile([P, C], F32)
-            nc.tensor.matmul(out=xp[:], lhsT=ident_bf[:], rhs=x_of[g][:, j, :], start=True, stop=True)
+            nc.tensor.matmul(out=xp[:, 0:cols], lhsT=ident_bf[:], rhs=x_of[g][:, j, 0:cols], start=True, stop=True)
             xp_of[g, j] = xp
 
-        def add_x_from_psum(g, j):
-            nc.vector.tensor_add(out=result_tile(g)[:, j, :], in0=xp_of[g, j][:], in1=shifted_of[g][:, j, :])
+        def add_x_on_vector(g, j, cols):
+            part = result_of[g][:, j, 0:cols]
+            nc.vector.tensor_add(out=part, in0=xp_of[g, j][:, 0:cols], in1=part)
 
-        def add_x_on_gpsimd(g, j):
-            nc.gpsimd.tensor_tensor(
-                out=result_tile(g)[:, j, :], in0=shifted_of[g][:, j, :], in1=x_of[g][:, j, :], op=ALU.add
+        def add_x_on_gpsimd(g, start, stop):
+            part = result_of[g][:].rearrange("p t c -> p (t c)")[:, start:stop]
+            x_part = x_of[g][:].rearrange("p t c -> p (t c)")[:, start:stop]
+            nc.gpsimd.tensor_tensor(out=part, in0=part, in1=x_part, op=ALU.add)
+
+        def shift_on_scalar(g, j):
+            nc.scalar.activation(
+                out=result_tile(g)[:, j, :],
+                in_=x_of[g][:, j, :],
+                func=ACT.Identity,
+                bias=offset_of[g][:, j : j + 1],
+                scale=1.0,
+            )
+
+        def shift_on_vector(g, j):
+            nc.vector.tensor_scalar_add(
+                out=result_tile(g)[:, j, :], in0=x_of[g][:, j, :], scalar1=offset_of[g][:, j : j + 1]
             )
 
         def finish(g, j):
             nc.vector.scalar_tensor_tensor(
-                out=result_tile(g)[:, j, :],
+                out=result_of[g][:, j, :],
                 in0=a_of[g][:, j, :],
                 scalar=gain_of[g][:, j : j + 1],
-                in1=shifted_of[g][:, j, :],
+                in1=result_of[g][:, j, :],
                 op0=ALU.mult,
                 op1=ALU.add,
             )
@@ -345,23 +324,8 @@ def tile_swintransformerblock_pb_t_kernel(
             if 0 <= g < GROUPS:
                 stage(g, *args)
 
-        def roles(g):
-            if g == GROUPS - 3:
-                return ["psum", "psum", "gpsimd", "scalar"]
-            if g > GROUPS - 3:
-                return ["vector", "scalar", "scalar", "scalar"]
-            return ["psum", "psum", "gpsimd", "scalar"] if g % 2 == 0 else ["psum", "shift", "gpsimd", "gpsimd"]
-
-        pending = []
-        left = {}
-
-        def tile_done(g, j):
-            if g == GROUPS - 1:
-                store(g, j)
-                return
-            left[g] -= 1
-            if left[g] == 0:
-                store(g)
+        THROUGH_PSUM = [(0, C), (1, PSUM_COLS - C)]
+        LOOP = GROUPS - 3
 
         for pair in range(TILES // 2):
             transposes(0, pair)
@@ -369,7 +333,6 @@ def tile_swintransformerblock_pb_t_kernel(
         spread_bias()
         scale_constants()
         load_o(3)
-        load_x(0)
         quantise(0, 0)
         quantise(0, 1)
         for pair in range(TILES // 2):
@@ -378,45 +341,33 @@ def tile_swintransformerblock_pb_t_kernel(
         for j in range(TILES):
             project(0, j)
         load_o(4)
-        load_x(1)
+        load_x(0)
         transposes(2, 0)
         transposes(2, 1)
 
-        for i in range(GROUPS + 2):
+        for i in range(GROUPS):
             run(load_o, i + O_LOAD_AHEAD)
             run(load_x, i + X_LOAD_AHEAD)
-            g = i - 2
-            role = roles(g) if g >= 0 else []
-            by = {r: [j for j in range(len(role)) if role[j] == r] for r in ("psum", "shift", "scalar", "gpsimd", "vector")}
-            left[g] = TILES
-            late = g >= GROUPS - 3
-
-            def last_pass(stage, j):
-                stage(g, j)
-                tile_done(g, j)
-
+            last = i == GROUPS - 1
+            scaled, added = i - 2, i - 3
             run(regroup, i + COPY_AHEAD, 0)
+            run(root, i - 1)
+            if added >= 0:
+                add_x_on_gpsimd(added, PSUM_COLS, TILES * C)
+            if scaled >= 0 and not last:
+                scale_on_scalar(scaled, 2)
             run(add_eps, i - 1)
-            if late:
-                for j in by["gpsimd"]:
-                    scale_a(g, j)
-                for j in by["scalar"]:
-                    shift_x(g, j)
-            for j in by["psum"]:
-                scale_a_on_gpsimd(g, j)
-            for j in by["shift"]:
-                shift_x_on_gpsimd(g, j)
-            if late:
-                pending += [(g, j) for j in by["gpsimd"]]
-            n = len(pending) if late else 2 if g % 2 == 0 else 1
-            for k, j in pending[:n]:
-                add_x_on_gpsimd(k, j)
-                tile_done(k, j)
-            pending = pending[n:]
-            if not late:
-                pending += [(g, j) for j in by["gpsimd"]]
+            run(regroup, i + COPY_AHEAD, 1)
+            if scaled >= 0 and not last:
+                scale_on_scalar(scaled, 3)
+            if last:
+                for j in (3, 0, 1):
+                    scale_on_scalar(scaled, j)
+                shift_on_scalar(scaled, 2)
+                add_x_on_gpsimd(scaled, 3 * C, 4 * C)
+                lay_x(scaled, 0, C)
             for j in range(TILES):
-                run(add_bias, i, j)
+                add_bias(i, j)
                 if i == 0 and j == 1:
                     quantise(1, 0)
                     quantise(1, 1)
@@ -424,37 +375,45 @@ def tile_swintransformerblock_pb_t_kernel(
                 run(project, i + 1, j)
                 if j == TILES - 1:
                     run(transposes, i + COPY_AHEAD + 1, 0)
-                run(square, i, j)
-                if j == 1:
-                    run(regroup, i + COPY_AHEAD, 1)
-                    if not late:
-                        for t in by["scalar"]:
-                            shift_x(g, t)
+                square(i, j)
             run(transposes, i + COPY_AHEAD + 1, 1)
-            if not late:
-                for t in by["gpsimd"]:
-                    scale_a(g, t)
-            run(root, i)
-            for j in by["vector"]:
-                shift_x_on_vector(g, j)
-            for j in by["psum"]:
-                last_pass(add_x_from_psum, j)
-            if 0 <= g + 1 < GROUPS - 2:
-                for j in range(TILES):
-                    if roles(g + 1)[j] == "psum":
-                        lay_x(g + 1, j)
+            if added >= 0:
+                for j, cols in THROUGH_PSUM:
+                    add_x_on_vector(added, j, cols)
+                store(added)
+            if last:
+                lay_x(scaled, 1, C)
+                for j in (0, 1):
+                    add_x_on_vector(scaled, j, C)
+            elif 0 <= added + 1 < LOOP:
+                for j, cols in THROUGH_PSUM:
+                    lay_x(added + 1, j, cols)
             run(chain, i - 1, 0)
-            run(chain, i - 1, 1)
             run(quantise, i + QUANTISE_AHEAD, 0)
-            from_sbuf = by["vector"] + by["scalar"] + by["shift"]
-            early = 1 if len(from_sbuf) > 1 else 0
-            for j in from_sbuf[:early]:
-                last_pass(finish, j)
+            run(chain, i - 1, 1)
+            if last:
+                finish(scaled, 2)
+                store(scaled)
+            elif scaled >= 0:
+                scale_on_vector(scaled, 0)
             run(chain, i - 1, 2)
+            if scaled >= 0 and not last:
+                scale_on_vector(scaled, 1)
             run(chain, i - 1, 3)
-            for j in from_sbuf[early : early + 1]:
-                last_pass(finish, j)
-            run(chain, i - 1, 4)
-            for j in from_sbuf[early + 1 :]:
-                last_pass(finish, j)
             run(quantise, i + QUANTISE_AHEAD, 1)
+
+        for g in (GROUPS - 2, GROUPS - 1):
+            run(root, g + 1)
+            run(add_eps, g + 1)
+            shift_on_vector(g, 0)
+            for j in range(1, TILES):
+                shift_on_scalar(g, j)
+            run(chain, g + 1, 0)
+            for j in range(TILES):
+                finish(g, j)
+                if g == GROUPS - 1:
+                    store(g, j)
+                if j < 3:
+                    run(chain, g + 1, j + 1)
+            if g < GROUPS - 1:
+                store(g)

@@ -27,7 +27,8 @@ QUANTISE_AHEAD = 2
 COPY_AHEAD = 2
 O_LOAD_AHEAD = 5
 X_LOAD_AHEAD = 1
-PSUM_COLS = 704
+PSUM_COLS = 640
+SPLIT = 128
 
 
 def tile_swintransformerblock_pb_t_kernel(
@@ -256,19 +257,19 @@ def tile_swintransformerblock_pb_t_kernel(
                 result_of[g] = result
             return result_of[g]
 
-        def scale_on_scalar(g, j):
+        def scale_on_scalar(g, j, start=0):
             nc.scalar.activation(
-                out=result_tile(g)[:, j, :],
-                in_=a_of[g][:, j, :],
+                out=result_tile(g)[:, j, start:C],
+                in_=a_of[g][:, j, start:C],
                 func=ACT.Identity,
                 bias=offset_of[g][:, j : j + 1],
                 scale=gain_of[g][:, j : j + 1],
             )
 
-        def scale_on_vector(g, j):
+        def scale_on_vector(g, j, stop=C):
             nc.vector.tensor_scalar(
-                out=result_tile(g)[:, j, :],
-                in0=a_of[g][:, j, :],
+                out=result_tile(g)[:, j, 0:stop],
+                in0=a_of[g][:, j, 0:stop],
                 scalar1=gain_of[g][:, j : j + 1],
                 scalar2=offset_of[g][:, j : j + 1],
                 op0=ALU.mult,
@@ -350,21 +351,21 @@ def tile_swintransformerblock_pb_t_kernel(
             run(load_x, i + X_LOAD_AHEAD)
             last = i == GROUPS - 1
             scaled, added = i - 2, i - 3
-            run(regroup, i + COPY_AHEAD, 0)
+            if i > 0:
+                run(regroup, i + COPY_AHEAD, 0)
             run(root, i - 1)
             if added >= 0:
                 add_x_on_gpsimd(added, PSUM_COLS, TILES * C)
             if scaled >= 0 and not last:
-                scale_on_scalar(scaled, 2)
+                scale_on_scalar(scaled, 2, SPLIT)
             run(add_eps, i - 1)
-            run(regroup, i + COPY_AHEAD, 1)
+            if i > 0:
+                run(regroup, i + COPY_AHEAD, 1)
             if scaled >= 0 and not last:
                 scale_on_scalar(scaled, 3)
             if last:
-                for j in (3, 0, 1):
+                for j in (0, 1):
                     scale_on_scalar(scaled, j)
-                shift_on_scalar(scaled, 2)
-                add_x_on_gpsimd(scaled, 3 * C, 4 * C)
                 lay_x(scaled, 0, C)
             for j in range(TILES):
                 add_bias(i, j)
@@ -376,44 +377,64 @@ def tile_swintransformerblock_pb_t_kernel(
                 if j == TILES - 1:
                     run(transposes, i + COPY_AHEAD + 1, 0)
                 square(i, j)
+                if i == 0 and j == 1:
+                    regroup(2, 0)
+                    regroup(2, 1)
             run(transposes, i + COPY_AHEAD + 1, 1)
             if added >= 0:
                 for j, cols in THROUGH_PSUM:
                     add_x_on_vector(added, j, cols)
                 store(added)
             if last:
-                lay_x(scaled, 1, C)
-                for j in (0, 1):
-                    add_x_on_vector(scaled, j, C)
-            elif 0 <= added + 1 < LOOP:
+                break
+            if 0 <= added + 1 < LOOP:
                 for j, cols in THROUGH_PSUM:
                     lay_x(added + 1, j, cols)
             run(chain, i - 1, 0)
             run(quantise, i + QUANTISE_AHEAD, 0)
             run(chain, i - 1, 1)
-            if last:
-                finish(scaled, 2)
-                store(scaled)
-            elif scaled >= 0:
+            if scaled >= 0:
                 scale_on_vector(scaled, 0)
             run(chain, i - 1, 2)
-            if scaled >= 0 and not last:
+            if scaled >= 0:
+                scale_on_vector(scaled, 2, SPLIT)
                 scale_on_vector(scaled, 1)
             run(chain, i - 1, 3)
             run(quantise, i + QUANTISE_AHEAD, 1)
 
-        for g in (GROUPS - 2, GROUPS - 1):
-            run(root, g + 1)
-            run(add_eps, g + 1)
-            shift_on_vector(g, 0)
-            for j in range(1, TILES):
-                shift_on_scalar(g, j)
-            run(chain, g + 1, 0)
-            for j in range(TILES):
-                finish(g, j)
-                if g == GROUPS - 1:
-                    store(g, j)
-                if j < 3:
-                    run(chain, g + 1, j + 1)
-            if g < GROUPS - 1:
-                store(g)
+        g = GROUPS - 3
+        lay_x(g, 1, C)
+        chain(g + 1, 0)
+        add_x_on_vector(g, 0, C)
+        chain(g + 1, 1)
+        add_x_on_vector(g, 1, C)
+        chain(g + 1, 2)
+        shift_on_vector(g, 2)
+        chain(g + 1, 3)
+        shift_on_vector(g, 3)
+        root(GROUPS - 1)
+        shift_on_scalar(g + 1, 1)
+        add_eps(GROUPS - 1)
+        for j in (2, 3):
+            finish(g, j)
+        store(g)
+        for j in (2, 3):
+            shift_on_scalar(g + 1, j)
+        g += 1
+        chain(g + 1, 0)
+        shift_on_vector(g, 0)
+        chain(g + 1, 1)
+        finish(g, 1)
+        chain(g + 1, 2)
+        finish(g, 0)
+        chain(g + 1, 3)
+        for j in (2, 3):
+            finish(g, j)
+        store(g)
+        g += 1
+        shift_on_vector(g, 0)
+        for j in (1, 2, 3):
+            shift_on_scalar(g, j)
+        for j in (1, 2, 0, 3):
+            finish(g, j)
+            store(g, j)

@@ -27,8 +27,7 @@ QUANTISE_AHEAD = 2
 COPY_AHEAD = 2
 O_LOAD_AHEAD = 5
 X_LOAD_AHEAD = 1
-PSUM_COLS = 640
-SPLIT = 128
+PSUM_COLS = 768
 
 
 def tile_swintransformerblock_pb_t_kernel(
@@ -257,19 +256,19 @@ def tile_swintransformerblock_pb_t_kernel(
                 result_of[g] = result
             return result_of[g]
 
-        def scale_on_scalar(g, j, start=0):
+        def scale_on_scalar(g, j):
             nc.scalar.activation(
-                out=result_tile(g)[:, j, start:C],
-                in_=a_of[g][:, j, start:C],
+                out=result_tile(g)[:, j, :],
+                in_=a_of[g][:, j, :],
                 func=ACT.Identity,
                 bias=offset_of[g][:, j : j + 1],
                 scale=gain_of[g][:, j : j + 1],
             )
 
-        def scale_on_vector(g, j, stop=C):
+        def scale_on_vector(g, j):
             nc.vector.tensor_scalar(
-                out=result_tile(g)[:, j, 0:stop],
-                in0=a_of[g][:, j, 0:stop],
+                out=result_tile(g)[:, j, :],
+                in0=a_of[g][:, j, :],
                 scalar1=gain_of[g][:, j : j + 1],
                 scalar2=offset_of[g][:, j : j + 1],
                 op0=ALU.mult,
@@ -357,7 +356,7 @@ def tile_swintransformerblock_pb_t_kernel(
             if added >= 0:
                 add_x_on_gpsimd(added, PSUM_COLS, TILES * C)
             if scaled >= 0 and not last:
-                scale_on_scalar(scaled, 2, SPLIT)
+                scale_on_scalar(scaled, 2)
             run(add_eps, i - 1)
             if i > 0:
                 run(regroup, i + COPY_AHEAD, 1)
@@ -397,7 +396,6 @@ def tile_swintransformerblock_pb_t_kernel(
                 scale_on_vector(scaled, 0)
             run(chain, i - 1, 2)
             if scaled >= 0:
-                scale_on_vector(scaled, 2, SPLIT)
                 scale_on_vector(scaled, 1)
             run(chain, i - 1, 3)
             run(quantise, i + QUANTISE_AHEAD, 1)

@@ -25,9 +25,9 @@ FLOPS = 2 * IMAGES * 1024 * C * C
 
 QUANTISE_AHEAD = 2
 COPY_AHEAD = 2
-O_LOAD_AHEAD = 5
-X_LOAD_AHEAD = 1
-PSUM_COLS = 768
+O_LOAD_AHEAD = 9
+X_LOAD_AHEAD = 7
+PSUM_COLS = 704
 
 
 def tile_swintransformerblock_pb_t_kernel(
@@ -42,8 +42,8 @@ def tile_swintransformerblock_pb_t_kernel(
     with ExitStack() as ctx:
         ctx.enter_context(tc.manual_schedule())
         const = ctx.enter_context(tc.tile_pool(name="const", bufs=1))
-        o_pool = ctx.enter_context(tc.tile_pool(name="o", bufs=5))
-        x_pool = ctx.enter_context(tc.tile_pool(name="x", bufs=7))
+        o_pool = ctx.enter_context(tc.tile_pool(name="o", bufs=9))
+        x_pool = ctx.enter_context(tc.tile_pool(name="x", bufs=12))
         mx_pool = ctx.enter_context(tc.tile_pool(name="mx", bufs=4))
         work = ctx.enter_context(tc.tile_pool(name="work", bufs=5))
         stats = ctx.enter_context(tc.tile_pool(name="stats", bufs=5))
@@ -77,6 +77,8 @@ def tile_swintransformerblock_pb_t_kernel(
 
         load_o(0, 0, TILES // 2)
 
+        zeros = const.tile([P, P], F32)
+        nc.vector.memset(zeros[:], 0.0)
         w_words = const.tile([P, 2 * C], U8, align_bytes=64)
         w_scales = const.tile([P, C], U8, align_bytes=64)
         nc.vector.memset(w_scales[:].bitcast(I32), 0)
@@ -127,6 +129,9 @@ def tile_swintransformerblock_pb_t_kernel(
         bias_s = const.tile([P, C], F32)
         ada_scale_s = const.tile([P, RUN], F32)
         bias_ps = y_pool.tile([P, C], F32, tag="y")
+
+        def keep_busy(out):
+            nc.tensor.matmul(out=out, lhsT=zeros[:], rhs=zeros[:], start=True, stop=True)
 
         def spread_bias():
             nc.tensor.matmul(out=bias_ps[:], lhsT=ones[:], rhs=bias_row[:], start=True, stop=True)
@@ -327,12 +332,18 @@ def tile_swintransformerblock_pb_t_kernel(
         THROUGH_PSUM = [(0, C), (1, PSUM_COLS - C)]
         LOOP = GROUPS - 3
 
+        for g in range(3, O_LOAD_AHEAD):
+            load_o(g)
+            load_x(g - 3)
+        load_x(X_LOAD_AHEAD - 1)
+
+        for k in range(4):
+            keep_busy(bias_ps[:, P * k : P * (k + 1)])
         for pair in range(TILES // 2):
             transposes(0, pair)
             regroup(0, pair)
         spread_bias()
         scale_constants()
-        load_o(3)
         quantise(0, 0)
         quantise(0, 1)
         for pair in range(TILES // 2):
@@ -340,8 +351,6 @@ def tile_swintransformerblock_pb_t_kernel(
             regroup(1, pair)
         for j in range(TILES):
             project(0, j)
-        load_o(4)
-        load_x(0)
         transposes(2, 0)
         transposes(2, 1)
 
@@ -389,6 +398,7 @@ def tile_swintransformerblock_pb_t_kernel(
             if 0 <= added + 1 < LOOP:
                 for j, cols in THROUGH_PSUM:
                     lay_x(added + 1, j, cols)
+                keep_busy(xp_of[added + 1, 1][:, 2 * P : 3 * P])
             run(chain, i - 1, 0)
             run(quantise, i + QUANTISE_AHEAD, 0)
             run(chain, i - 1, 1)

@@ -77,8 +77,6 @@ def tile_swintransformerblock_pb_t_kernel(
 
         load_o(0, 0, TILES // 2)
 
-        zeros = const.tile([P, P], F32)
-        nc.vector.memset(zeros[:], 0.0)
         w_words = const.tile([P, 2 * C], U8, align_bytes=64)
         w_scales = const.tile([P, C], U8, align_bytes=64)
         nc.vector.memset(w_scales[:].bitcast(I32), 0)
@@ -129,9 +127,6 @@ def tile_swintransformerblock_pb_t_kernel(
         bias_s = const.tile([P, C], F32)
         ada_scale_s = const.tile([P, RUN], F32)
         bias_ps = y_pool.tile([P, C], F32, tag="y")
-
-        def keep_busy(out):
-            nc.tensor.matmul(out=out, lhsT=zeros[:], rhs=zeros[:], start=True, stop=True)
 
         def spread_bias():
             nc.tensor.matmul(out=bias_ps[:], lhsT=ones[:], rhs=bias_row[:], start=True, stop=True)
@@ -337,8 +332,6 @@ def tile_swintransformerblock_pb_t_kernel(
             load_x(g - 3)
         load_x(X_LOAD_AHEAD - 1)
 
-        for k in range(4):
-            keep_busy(bias_ps[:, P * k : P * (k + 1)])
         for pair in range(TILES // 2):
             transposes(0, pair)
             regroup(0, pair)
@@ -362,7 +355,10 @@ def tile_swintransformerblock_pb_t_kernel(
             if i > 0:
                 run(regroup, i + COPY_AHEAD, 0)
             run(root, i - 1)
-            if added >= 0:
+            if last:
+                add_x_on_gpsimd(added, PSUM_COLS, 3 * C)
+                add_x_on_gpsimd(added, 3 * C, 4 * C)
+            elif added >= 0:
                 add_x_on_gpsimd(added, PSUM_COLS, TILES * C)
             if scaled >= 0 and not last:
                 scale_on_scalar(scaled, 2)
@@ -392,13 +388,16 @@ def tile_swintransformerblock_pb_t_kernel(
             if added >= 0:
                 for j, cols in THROUGH_PSUM:
                     add_x_on_vector(added, j, cols)
-                store(added)
+                if last:
+                    for j in (0, 2, 1, 3):
+                        store(added, j)
+                else:
+                    store(added)
             if last:
                 break
             if 0 <= added + 1 < LOOP:
                 for j, cols in THROUGH_PSUM:
                     lay_x(added + 1, j, cols)
-                keep_busy(xp_of[added + 1, 1][:, 2 * P : 3 * P])
             run(chain, i - 1, 0)
             run(quantise, i + QUANTISE_AHEAD, 0)
             run(chain, i - 1, 1)
@@ -414,8 +413,10 @@ def tile_swintransformerblock_pb_t_kernel(
         lay_x(g, 1, C)
         chain(g + 1, 0)
         add_x_on_vector(g, 0, C)
+        store(g, 0)
         chain(g + 1, 1)
         add_x_on_vector(g, 1, C)
+        store(g, 1)
         chain(g + 1, 2)
         shift_on_vector(g, 2)
         chain(g + 1, 3)
@@ -425,7 +426,7 @@ def tile_swintransformerblock_pb_t_kernel(
         add_eps(GROUPS - 1)
         for j in (2, 3):
             finish(g, j)
-        store(g)
+            store(g, j)
         for j in (2, 3):
             shift_on_scalar(g + 1, j)
         g += 1
@@ -433,12 +434,14 @@ def tile_swintransformerblock_pb_t_kernel(
         shift_on_vector(g, 0)
         chain(g + 1, 1)
         finish(g, 1)
+        store(g, 1)
         chain(g + 1, 2)
         finish(g, 0)
+        store(g, 0)
         chain(g + 1, 3)
         for j in (2, 3):
             finish(g, j)
-        store(g)
+            store(g, j)
         g += 1
         shift_on_vector(g, 0)
         for j in (1, 2, 3):

@@ -27,7 +27,7 @@ QUANTISE_AHEAD = 2
 COPY_AHEAD = 2
 O_LOAD_AHEAD = 9
 X_LOAD_AHEAD = 7
-PSUM_COLS = 704
+PSUM_COLS = 640
 
 
 def tile_swintransformerblock_pb_t_kernel(
@@ -352,25 +352,34 @@ def tile_swintransformerblock_pb_t_kernel(
             run(load_x, i + X_LOAD_AHEAD)
             last = i == GROUPS - 1
             scaled, added = i - 2, i - 3
+            scalar_tiles = (0, 1) if last else (2, 3)
+            no_copies = i >= GROUPS - 1
             if i > 0:
                 run(regroup, i + COPY_AHEAD, 0)
-            run(root, i - 1)
-            if last:
-                add_x_on_gpsimd(added, PSUM_COLS, 3 * C)
-                add_x_on_gpsimd(added, 3 * C, 4 * C)
-            elif added >= 0:
-                add_x_on_gpsimd(added, PSUM_COLS, TILES * C)
-            if scaled >= 0 and not last:
-                scale_on_scalar(scaled, 2)
+            if not no_copies:
+                run(root, i - 1)
+            if scaled >= 0:
+                scale_on_scalar(scaled, scalar_tiles[0])
+            if no_copies:
+                root(i - 1)
+            if no_copies:
+                scale_on_scalar(scaled, scalar_tiles[1])
             run(add_eps, i - 1)
             if i > 0:
                 run(regroup, i + COPY_AHEAD, 1)
-            if scaled >= 0 and not last:
-                scale_on_scalar(scaled, 3)
+            if scaled >= 0 and not no_copies:
+                scale_on_scalar(scaled, scalar_tiles[1])
             if last:
-                for j in (0, 1):
-                    scale_on_scalar(scaled, j)
+                for j, cols in THROUGH_PSUM:
+                    add_x_on_vector(added, j, cols)
+                store(added, 0)
+                for start, stop in ((PSUM_COLS, 3 * C), (3 * C, 4 * C)):
+                    add_x_on_gpsimd(added, start, stop)
+                    for j in range(max(1, start // C), stop // C):
+                        store(added, j)
                 lay_x(scaled, 0, C)
+            elif added >= 0:
+                add_x_on_gpsimd(added, PSUM_COLS, TILES * C)
             for j in range(TILES):
                 add_bias(i, j)
                 if i == 0 and j == 1:
@@ -385,16 +394,12 @@ def tile_swintransformerblock_pb_t_kernel(
                     regroup(2, 0)
                     regroup(2, 1)
             run(transposes, i + COPY_AHEAD + 1, 1)
+            if last:
+                break
             if added >= 0:
                 for j, cols in THROUGH_PSUM:
                     add_x_on_vector(added, j, cols)
-                if last:
-                    for j in (0, 2, 1, 3):
-                        store(added, j)
-                else:
-                    store(added)
-            if last:
-                break
+                store(added)
             if 0 <= added + 1 < LOOP:
                 for j, cols in THROUGH_PSUM:
                     lay_x(added + 1, j, cols)

@@ -85,10 +85,10 @@ def tile_swintransformerblock_pb_t_kernel(
                 out=w_scales[32 * quadrant : 32 * quadrant + 4, :].bitcast(I32),
                 in_=out_w_scales[0, 4 * quadrant : 4 * quadrant + 4, :].bitcast(I32),
             )
-        nc.sync.dma_start(out=w_words[:].bitcast(I32), in_=out_w_words[0].bitcast(I32))
         load_o(0, TILES // 2, TILES // 2)
-        for g in range(1, 3):
-            load_o(g)
+        load_o(1)
+        nc.sync.dma_start(out=w_words[:].bitcast(I32), in_=out_w_words[0].bitcast(I32))
+        load_o(2)
 
         bias_row = const.tile([P, C], BF16)
         nc.vector.memset(bias_row[:], 0.0)
@@ -354,7 +354,7 @@ def tile_swintransformerblock_pb_t_kernel(
             scaled, added = i - 2, i - 3
             scalar_tiles = (0, 1) if last else (2, 3)
             no_copies = i >= GROUPS - 1
-            if i > 0:
+            if i > 1:
                 run(regroup, i + COPY_AHEAD, 0)
             if not no_copies:
                 run(root, i - 1)
@@ -364,8 +364,8 @@ def tile_swintransformerblock_pb_t_kernel(
                 root(i - 1)
             if no_copies:
                 scale_on_scalar(scaled, scalar_tiles[1])
-            run(add_eps, i - 1)
-            if i > 0:
+            if i > 1:
+                run(add_eps, i - 1)
                 run(regroup, i + COPY_AHEAD, 1)
             if scaled >= 0 and not no_copies:
                 scale_on_scalar(scaled, scalar_tiles[1])
@@ -390,9 +390,11 @@ def tile_swintransformerblock_pb_t_kernel(
                 if j == TILES - 1:
                     run(transposes, i + COPY_AHEAD + 1, 0)
                 square(i, j)
-                if i == 0 and j == 1:
-                    regroup(2, 0)
-                    regroup(2, 1)
+                if i < 2 and j == 0:
+                    run(add_eps, i - 1)
+                if (i, j) in ((0, 1), (1, 0)):
+                    regroup(i + 2, 0)
+                    regroup(i + 2, 1)
             run(transposes, i + COPY_AHEAD + 1, 1)
             if last:
                 break

@@ -25,8 +25,7 @@ FLOPS = 2 * IMAGES * 1024 * C * C
 
 QUANTISE_AHEAD = 2
 COPY_AHEAD = 2
-O_LOAD_AHEAD = 9
-X_LOAD_AHEAD = 7
+O_IMAGES = 4
 PSUM_COLS = 640
 
 
@@ -42,8 +41,8 @@ def tile_swintransformerblock_pb_t_kernel(
     with ExitStack() as ctx:
         ctx.enter_context(tc.manual_schedule())
         const = ctx.enter_context(tc.tile_pool(name="const", bufs=1))
-        o_pool = ctx.enter_context(tc.tile_pool(name="o", bufs=9))
-        x_pool = ctx.enter_context(tc.tile_pool(name="x", bufs=12))
+        o_pool = ctx.enter_context(tc.tile_pool(name="o", bufs=5))
+        x_pool = ctx.enter_context(tc.tile_pool(name="x", bufs=6))
         mx_pool = ctx.enter_context(tc.tile_pool(name="mx", bufs=4))
         work = ctx.enter_context(tc.tile_pool(name="work", bufs=5))
         stats = ctx.enter_context(tc.tile_pool(name="stats", bufs=5))
@@ -59,21 +58,23 @@ def tile_swintransformerblock_pb_t_kernel(
             b, hc = divmod(g, 2)
             return b, hc, 1 - hc
 
-        def load_o(g, first=0, count=TILES):
-            b, hc, ht = place(g)
-            if g not in o_of:
-                o_sb = o_pool.tile([P, TILES, C], BF16)
-                o_of[g] = o_sb
+        def load_o(b, first=0, count=RUN):
+            if b not in o_of:
+                o_sb = o_pool.tile([P, RUN, C], BF16)
+                o_of[b] = o_sb
             nc.sync.dma_start(
-                out=o_of[g][:, first : first + count, :],
-                in_=o_rows[P * b : P * (b + 1), TILES * hc + first : TILES * hc + first + count, :],
+                out=o_of[b][:, first : first + count, :],
+                in_=o_rows[P * b : P * (b + 1), first : first + count, :],
             )
 
-        def load_x(g):
+        def load_x(b):
+            x_sb = x_pool.tile([P, RUN, C], BF16)
+            nc.sync.dma_start(out=x_sb[:], in_=x_rows[b])
+            x_of[b] = x_sb
+
+        def x_tile(g, j):
             b, hc, ht = place(g)
-            x_sb = x_pool.tile([P, TILES, C], BF16)
-            nc.sync.dma_start(out=x_sb[:], in_=x_rows[b, :, TILES * ht : TILES * (ht + 1), :])
-            x_of[g] = x_sb
+            return x_of[b][:, TILES * ht + j, :]
 
         load_o(0, 0, TILES // 2)
 
@@ -86,9 +87,10 @@ def tile_swintransformerblock_pb_t_kernel(
                 in_=out_w_scales[0, 4 * quadrant : 4 * quadrant + 4, :].bitcast(I32),
             )
         load_o(0, TILES // 2, TILES // 2)
-        load_o(1)
+        load_o(0, TILES, TILES)
         nc.sync.dma_start(out=w_words[:].bitcast(I32), in_=out_w_words[0].bitcast(I32))
-        load_o(2)
+        load_o(1, 0, TILES)
+        load_o(1, TILES, TILES)
 
         bias_row = const.tile([P, C], BF16)
         nc.vector.memset(bias_row[:], 0.0)
@@ -139,13 +141,13 @@ def tile_swintransformerblock_pb_t_kernel(
 
         def transposes(g, pair):
             b, hc, ht = place(g)
-            o_words = o_of[g][:].bitcast(F32)
+            o_words = o_of[b][:].bitcast(F32)
             tp = tp_pool.tile([P, 2, 2 * P], F32)
             for half in range(2):
                 for u in range(2):
                     nc.tensor.transpose(
                         tp[:, u, P * half : P * (half + 1)],
-                        o_words[:, 2 * pair + half, u : C // 2 : 2],
+                        o_words[:, TILES * hc + 2 * pair + half, u : C // 2 : 2],
                         perm[hc][:],
                     )
             tp_of[g, pair] = tp
@@ -277,7 +279,7 @@ def tile_swintransformerblock_pb_t_kernel(
 
         def lay_x(g, j, cols):
             xp = xp_pool.tile([P, C], F32)
-            nc.tensor.matmul(out=xp[:, 0:cols], lhsT=ident_bf[:], rhs=x_of[g][:, j, 0:cols], start=True, stop=True)
+            nc.tensor.matmul(out=xp[:, 0:cols], lhsT=ident_bf[:], rhs=x_tile(g, j)[:, 0:cols], start=True, stop=True)
             xp_of[g, j] = xp
 
         def add_x_on_vector(g, j, cols):
@@ -286,13 +288,15 @@ def tile_swintransformerblock_pb_t_kernel(
 
         def add_x_on_gpsimd(g, start, stop):
             part = result_of[g][:].rearrange("p t c -> p (t c)")[:, start:stop]
-            x_part = x_of[g][:].rearrange("p t c -> p (t c)")[:, start:stop]
+            b, hc, ht = place(g)
+            x_first = TILES * C * ht
+            x_part = x_of[b][:].rearrange("p t c -> p (t c)")[:, x_first + start : x_first + stop]
             nc.gpsimd.tensor_tensor(out=part, in0=part, in1=x_part, op=ALU.add)
 
         def shift_on_scalar(g, j):
             nc.scalar.activation(
                 out=result_tile(g)[:, j, :],
-                in_=x_of[g][:, j, :],
+                in_=x_tile(g, j),
                 func=ACT.Identity,
                 bias=offset_of[g][:, j : j + 1],
                 scale=1.0,
@@ -300,7 +304,7 @@ def tile_swintransformerblock_pb_t_kernel(
 
         def shift_on_vector(g, j):
             nc.vector.tensor_scalar_add(
-                out=result_tile(g)[:, j, :], in0=x_of[g][:, j, :], scalar1=offset_of[g][:, j : j + 1]
+                out=result_tile(g)[:, j, :], in0=x_tile(g, j), scalar1=offset_of[g][:, j : j + 1]
             )
 
         def finish(g, j):
@@ -313,12 +317,15 @@ def tile_swintransformerblock_pb_t_kernel(
                 op1=ALU.add,
             )
 
-        def store(g, j=None):
+        def store(g, j=None, count=1):
             b, hc, ht = place(g)
             if j is None:
                 nc.sync.dma_start(out=out_rows[b, :, TILES * ht : TILES * (ht + 1), :], in_=result_of[g][:])
             else:
-                nc.sync.dma_start(out=out_rows[b, :, TILES * ht + j, :], in_=result_of[g][:, j, :])
+                nc.sync.dma_start(
+                    out=out_rows[b, :, TILES * ht + j : TILES * ht + j + count, :],
+                    in_=result_of[g][:, j : j + count, :],
+                )
 
         def run(stage, g, *args):
             if 0 <= g < GROUPS:
@@ -327,10 +334,10 @@ def tile_swintransformerblock_pb_t_kernel(
         THROUGH_PSUM = [(0, C), (1, PSUM_COLS - C)]
         LOOP = GROUPS - 3
 
-        for g in range(3, O_LOAD_AHEAD):
-            load_o(g)
-            load_x(g - 3)
-        load_x(X_LOAD_AHEAD - 1)
+        load_x(0)
+        for b in range(2, O_IMAGES):
+            load_o(b)
+            load_x(b - 1)
 
         for pair in range(TILES // 2):
             transposes(0, pair)
@@ -348,8 +355,11 @@ def tile_swintransformerblock_pb_t_kernel(
         transposes(2, 1)
 
         for i in range(GROUPS):
-            run(load_o, i + O_LOAD_AHEAD)
-            run(load_x, i + X_LOAD_AHEAD)
+            if i % 2 == 0:
+                if i // 2 + O_IMAGES < IMAGES:
+                    load_o(i // 2 + O_IMAGES)
+                if i // 2 + O_IMAGES - 1 < IMAGES:
+                    load_x(i // 2 + O_IMAGES - 1)
             last = i == GROUPS - 1
             scaled, added = i - 2, i - 3
             scalar_tiles = (0, 1) if last else (2, 3)
@@ -375,8 +385,8 @@ def tile_swintransformerblock_pb_t_kernel(
                 store(added, 0)
                 for start, stop in ((PSUM_COLS, 3 * C), (3 * C, 4 * C)):
                     add_x_on_gpsimd(added, start, stop)
-                    for j in range(max(1, start // C), stop // C):
-                        store(added, j)
+                    first = max(1, start // C)
+                    store(added, first, stop // C - first)
                 lay_x(scaled, 0, C)
             elif added >= 0:
                 add_x_on_gpsimd(added, PSUM_COLS, TILES * C)
@@ -420,10 +430,9 @@ def tile_swintransformerblock_pb_t_kernel(
         lay_x(g, 1, C)
         chain(g + 1, 0)
         add_x_on_vector(g, 0, C)
-        store(g, 0)
         chain(g + 1, 1)
         add_x_on_vector(g, 1, C)
-        store(g, 1)
+        store(g, 0, 2)
         chain(g + 1, 2)
         shift_on_vector(g, 2)
         chain(g + 1, 3)
@@ -434,19 +443,20 @@ def tile_swintransformerblock_pb_t_kernel(
         for j in (2, 3):
             finish(g, j)
             store(g, j)
-        for j in (2, 3):
+        for j in (2, 3, 0):
             shift_on_scalar(g + 1, j)
         g += 1
         chain(g + 1, 0)
-        shift_on_vector(g, 0)
-        chain(g + 1, 1)
         finish(g, 1)
         store(g, 1)
+        chain(g + 1, 1)
+        finish(g, 2)
+        store(g, 2)
         chain(g + 1, 2)
-        finish(g, 0)
-        store(g, 0)
+        finish(g, 3)
+        store(g, 3)
         chain(g + 1, 3)
-        for j in (2, 3):
+        for j in (0,):
             finish(g, j)
             store(g, j)
         g += 1

from contextlib import ExitStack

import concourse.mybir as mybir
from concourse.masks import make_identity

F32 = mybir.dt.float32
BF16 = mybir.dt.bfloat16
I32 = mybir.dt.int32
U32 = mybir.dt.uint32
U8 = mybir.dt.uint8
FP8X4 = mybir.dt.float8_e4m3fn_x4
FP4X4 = mybir.dt.float4_e2m1fn_x4
ALU = mybir.AluOpType
ACT = mybir.ActivationFunctionType

P = 128
C = 512
IMAGES = 8
RUN = 8
TILES = 4
GROUPS = IMAGES * RUN // TILES
EPS = 1e-5

FLOPS = 2 * IMAGES * 1024 * C * C

QUANTISE_AHEAD = 2
COPY_AHEAD = 2
O_IMAGES = 4
PSUM_COLS = 640


def tile_swintransformerblock_pb_t_kernel(
    tc, o_attn, out_w_words, out_w_scales, out_b, ada1_scale, ada1_shift, x, out
):
    nc = tc.nc

    o_rows = o_attn.rearrange("w (r c) k -> (w r) c k", c=RUN)
    x_rows = x.rearrange("b (m t) k -> b m t k", t=RUN)
    out_rows = out.rearrange("b (m t) k -> b m t k", t=RUN)

    with ExitStack() as ctx:
        ctx.enter_context(tc.manual_schedule())
        const = ctx.enter_context(tc.tile_pool(name="const", bufs=1))
        o_pool = ctx.enter_context(tc.tile_pool(name="o", bufs=5))
        x_pool = ctx.enter_context(tc.tile_pool(name="x", bufs=6))
        mx_pool = ctx.enter_context(tc.tile_pool(name="mx", bufs=4))
        work = ctx.enter_context(tc.tile_pool(name="work", bufs=5))
        stats = ctx.enter_context(tc.tile_pool(name="stats", bufs=5))
        tp_pool = ctx.enter_context(tc.psum_pool(name="tp", bufs=2))
        xp_pool = ctx.enter_context(tc.psum_pool(name="xp", bufs=2))
        y_pool = ctx.enter_context(tc.psum_pool(name="y", bufs=4))

        o_of, x_of, grouped_of, codes_of, scales_of, y_of = {}, {}, {}, {}, {}, {}
        a_of, negmean_of, sumsq_of, std_of, gain_of, offset_of = {}, {}, {}, {}, {}, {}
        tp_of, denom_of, recip_of, centre_of, result_of, xp_of = {}, {}, {}, {}, {}, {}

        def place(g):
            b, hc = divmod(g, 2)
            return b, hc, 1 - hc

        def load_o(b, first=0, count=RUN):
            if b not in o_of:
                o_sb = o_pool.tile([P, RUN, C], BF16)
                o_of[b] = o_sb
            nc.sync.dma_start(
                out=o_of[b][:, first : first + count, :],
                in_=o_rows[P * b : P * (b + 1), first : first + count, :],
            )

        def load_x(b):
            x_sb = x_pool.tile([P, RUN, C], BF16)
            nc.sync.dma_start(out=x_sb[:], in_=x_rows[b])
            x_of[b] = x_sb

        def x_tile(g, j):
            b, hc, ht = place(g)
            return x_of[b][:, TILES * ht + j, :]

        load_o(0, 0, TILES // 2)

        w_words = const.tile([P, 2 * C], U8, align_bytes=64)
        w_scales = const.tile([P, C], U8, align_bytes=64)
        nc.vector.memset(w_scales[:].bitcast(I32), 0)
        for quadrant in range(4):
            nc.sync.dma_start(
                out=w_scales[32 * quadrant : 32 * quadrant + 4, :].bitcast(I32),
                in_=out_w_scales[0, 4 * quadrant : 4 * quadrant + 4, :].bitcast(I32),
            )
        load_o(0, TILES // 2, TILES // 2)
        load_o(0, TILES, TILES)
        nc.sync.dma_start(out=w_words[:].bitcast(I32), in_=out_w_words[0].bitcast(I32))
        load_o(1, 0, TILES)
        load_o(1, TILES, TILES)

        bias_row = const.tile([P, C], BF16)
        nc.vector.memset(bias_row[:], 0.0)
        nc.scalar.dma_start(out=bias_row[0:1, :], in_=out_b.rearrange("(u c) -> u c", u=1))
        ones = const.tile([P, P], BF16)
        nc.vector.memset(ones[:], -1.0 / C)
        ada_scale_sb = const.tile([P, RUN], BF16)
        nc.scalar.dma_start(out=ada_scale_sb[:], in_=ada1_scale[0].rearrange("(m t) u -> m (t u)", t=RUN))
        ada_shift_sb = const.tile([P, RUN], BF16)
        nc.scalar.dma_start(out=ada_shift_sb[:], in_=ada1_shift[0].rearrange("(m t) u -> m (t u)", t=RUN))
        warm = const.tile([P, 2], F32)
        nc.vector.memset(warm[:, 0:1], 1.0)
        nc.scalar.activation(out=warm[:, 1:2], in_=warm[:, 0:1], func=ACT.Sqrt)

        ident = const.tile([P, P], F32)
        make_identity(nc, ident[:])
        perm_lo = const.tile([P, P], F32)
        nc.vector.tensor_copy(
            out=perm_lo[:, 16:112].rearrange("q (wi r j) -> q wi r j", wi=3, r=8),
            in_=ident[:, 0:96].rearrange("q (wi j r) -> q wi r j", wi=3, j=4),
        )
        last_windows = ident[:, 96:128].rearrange("q (j r) -> q r j", j=4)
        nc.vector.tensor_copy(out=perm_lo[:, 112:128].rearrange("q (r j) -> q r j", r=4), in_=last_windows[:, 0:4, :])
        nc.vector.tensor_copy(out=perm_lo[:, 0:16].rearrange("q (r j) -> q r j", r=4), in_=last_windows[:, 4:8, :])
        perm_hi = const.tile([P, P], F32)
        lo_ij = perm_lo[:].rearrange("q (i j) -> q i j", j=4)
        hi_ij = perm_hi[:].rearrange("q (i j) -> q i j", j=4)
        nc.vector.tensor_copy(out=hi_ij[:, :, 1:4], in_=lo_ij[:, :, 0:3])
        nc.vector.tensor_copy(out=hi_ij[:, :, 0:1], in_=lo_ij[:, :, 3:4])
        perm = [perm_lo, perm_hi]
        ident_bf = const.tile([P, P], BF16)
        nc.vector.tensor_copy(out=ident_bf[:], in_=ident[:])

        squares = const.tile([P, TILES, C], BF16)

        bias_s = const.tile([P, C], F32)
        ada_scale_s = const.tile([P, RUN], F32)
        bias_ps = y_pool.tile([P, C], F32, tag="y")

        def spread_bias():
            nc.tensor.matmul(out=bias_ps[:], lhsT=ones[:], rhs=bias_row[:], start=True, stop=True)

        def scale_constants():
            nc.scalar.copy(out=bias_s[:], in_=bias_ps[:])
            nc.gpsimd.tensor_scalar(
                out=ada_scale_s[:], in0=ada_scale_sb[:], scalar1=-1.0 * C, scalar2=0.0, op0=ALU.mult, op1=ALU.add
            )

        def transposes(g, pair):
            b, hc, ht = place(g)
            o_words = o_of[b][:].bitcast(F32)
            tp = tp_pool.tile([P, 2, 2 * P], F32)
            for half in range(2):
                for u in range(2):
                    nc.tensor.transpose(
                        tp[:, u, P * half : P * (half + 1)],
                        o_words[:, TILES * hc + 2 * pair + half, u : C // 2 : 2],
                        perm[hc][:],
                    )
            tp_of[g, pair] = tp

        def regroup(g, pair):
            if pair == 0:
                grouped = mx_pool.tile([P, TILES * P * 4], BF16, align_bytes=64)
                grouped_of[g] = grouped
            grouped_words = grouped_of[g][:].bitcast(F32).rearrange("p (n u) -> p n u", u=2)
            nc.scalar.copy(
                out=grouped_words[:, 2 * P * pair : 2 * P * (pair + 1), :],
                in_=tp_of[g, pair][:].rearrange("p u n -> p n u"),
            )

        def quantise(g, pair):
            if pair == 0:
                codes = mx_pool.tile([P, TILES * P], U32, align_bytes=64)
                scales = mx_pool.tile([P, TILES * P], U8, align_bytes=64)
                codes_of[g], scales_of[g] = codes, scales
            cols = slice(2 * P * pair, 2 * P * (pair + 1))
            nc.vector.quantize_mx(
                out=codes_of[g][:, cols].bitcast(FP8X4),
                scales=scales_of[g][:, cols],
                in_=grouped_of[g][:, 8 * P * pair : 8 * P * (pair + 1)],
            )

        def project(g, j):
            y = y_pool.tile([P, C], F32, tag="y")
            nc.tensor.matmul_mx(
                out=y[:],
                lhsT=codes_of[g][:, P * j : P * (j + 1)].bitcast(FP8X4),
                lhsT_scale=scales_of[g][:, P * j : P * (j + 1)],
                rhs=w_words[:].bitcast(FP4X4),
                rhs_scale=w_scales[:],
                start=True,
                stop=True,
            )
            y_of[g, j] = y

        def add_bias(g, j):
            if j == 0:
                a = work.tile([P, TILES, C], F32)
                negmean = stats.tile([P, TILES], F32)
                a_of[g], negmean_of[g] = a, negmean
            nc.vector.scalar_tensor_tensor(
                out=a_of[g][:, j, :],
                in0=y_of[g, j][:],
                scalar=-1.0 / C,
                in1=bias_s[:],
                op0=ALU.mult,
                op1=ALU.add,
                accum_out=negmean_of[g][:, j : j + 1],
            )

        def square(g, j):
            if j == 0:
                sumsq = stats.tile([P, TILES], F32)
                sumsq_of[g] = sumsq
            nc.scalar.activation(
                out=squares[:, j, :],
                in_=a_of[g][:, j, :],
                func=ACT.Square,
                bias=negmean_of[g][:, j : j + 1],
                scale=-1.0 * C,
                accum_out=sumsq_of[g][:, j : j + 1],
            )

        def root(g):
            std = stats.tile([P, TILES], F32)
            nc.scalar.activation(out=std[:], in_=sumsq_of[g][:], func=ACT.Sqrt, scale=1.0 / (C - 1))
            std_of[g] = std

        def add_eps(g):
            denom = stats.tile([P, TILES], F32)
            nc.scalar.activation(out=denom[:], in_=std_of[g][:], func=ACT.Identity, bias=EPS, scale=1.0)
            denom_of[g] = denom

        def chain(g, step):
            b, hc, ht = place(g)
            tiles_of_image = slice(TILES * ht, TILES * (ht + 1))
            if step == 0:
                recip = stats.tile([P, TILES], F32)
                nc.vector.reciprocal(out=recip[:], in_=denom_of[g][:])
                recip_of[g] = recip
            elif step == 1:
                gain = stats.tile([P, TILES], F32)
                nc.vector.tensor_mul(out=gain[:], in0=recip_of[g][:], in1=ada_scale_s[:, tiles_of_image])
                gain_of[g] = gain
            elif step == 2:
                centre = stats.tile([P, TILES], F32)
                nc.vector.scalar_tensor_tensor(
                    out=centre[:],
                    in0=negmean_of[g][:],
                    scalar=-1.0 / C,
                    in1=gain_of[g][:],
                    op0=ALU.mult,
                    op1=ALU.mult,
                )
                centre_of[g] = centre
            else:
                offset = stats.tile([P, TILES], F32)
                nc.vector.tensor_add(out=offset[:], in0=centre_of[g][:], in1=ada_shift_sb[:, tiles_of_image])
                offset_of[g] = offset

        def result_tile(g):
            if g not in result_of:
                result = work.tile([P, TILES, C], F32)
                result_of[g] = result
            return result_of[g]

        def scale_on_scalar(g, j):
            nc.scalar.activation(
                out=result_tile(g)[:, j, :],
                in_=a_of[g][:, j, :],
                func=ACT.Identity,
                bias=offset_of[g][:, j : j + 1],
                scale=gain_of[g][:, j : j + 1],
            )

        def scale_on_vector(g, j):
            nc.vector.tensor_scalar(
                out=result_tile(g)[:, j, :],
                in0=a_of[g][:, j, :],
                scalar1=gain_of[g][:, j : j + 1],
                scalar2=offset_of[g][:, j : j + 1],
                op0=ALU.mult,
                op1=ALU.add,
            )

        def lay_x(g, j, cols):
            xp = xp_pool.tile([P, C], F32)
            nc.tensor.matmul(out=xp[:, 0:cols], lhsT=ident_bf[:], rhs=x_tile(g, j)[:, 0:cols], start=True, stop=True)
            xp_of[g, j] = xp

        def add_x_on_vector(g, j, cols):
            part = result_of[g][:, j, 0:cols]
            nc.vector.tensor_add(out=part, in0=xp_of[g, j][:, 0:cols], in1=part)

        def add_x_on_gpsimd(g, start, stop):
            part = result_of[g][:].rearrange("p t c -> p (t c)")[:, start:stop]
            b, hc, ht = place(g)
            x_first = TILES * C * ht
            x_part = x_of[b][:].rearrange("p t c -> p (t c)")[:, x_first + start : x_first + stop]
            nc.gpsimd.tensor_tensor(out=part, in0=part, in1=x_part, op=ALU.add)

        def shift_on_scalar(g, j):
            nc.scalar.activation(
                out=result_tile(g)[:, j, :],
                in_=x_tile(g, j),
                func=ACT.Identity,
                bias=offset_of[g][:, j : j + 1],
                scale=1.0,
            )

        def shift_on_vector(g, j):
            nc.vector.tensor_scalar_add(
                out=result_tile(g)[:, j, :], in0=x_tile(g, j), scalar1=offset_of[g][:, j : j + 1]
            )

        def finish(g, j):
            nc.vector.scalar_tensor_tensor(
                out=result_of[g][:, j, :],
                in0=a_of[g][:, j, :],
                scalar=gain_of[g][:, j : j + 1],
                in1=result_of[g][:, j, :],
                op0=ALU.mult,
                op1=ALU.add,
            )

        def store(g, j=None, count=1):
            b, hc, ht = place(g)
            if j is None:
                nc.sync.dma_start(out=out_rows[b, :, TILES * ht : TILES * (ht + 1), :], in_=result_of[g][:])
            else:
                nc.sync.dma_start(
                    out=out_rows[b, :, TILES * ht + j : TILES * ht + j + count, :],
                    in_=result_of[g][:, j : j + count, :],
                )

        def run(stage, g, *args):
            if 0 <= g < GROUPS:
                stage(g, *args)

        THROUGH_PSUM = [(0, C), (1, PSUM_COLS - C)]
        LOOP = GROUPS - 3

        load_x(0)
        for b in range(2, O_IMAGES):
            load_o(b)
            load_x(b - 1)

        for pair in range(TILES // 2):
            transposes(0, pair)
            regroup(0, pair)
        spread_bias()
        scale_constants()
        quantise(0, 0)
        quantise(0, 1)
        for pair in range(TILES // 2):
            transposes(1, pair)
            regroup(1, pair)
        for j in range(TILES):
            project(0, j)
        transposes(2, 0)
        transposes(2, 1)

        for i in range(GROUPS):
            if i % 2 == 0:
                if i // 2 + O_IMAGES < IMAGES:
                    load_o(i // 2 + O_IMAGES)
                if i // 2 + O_IMAGES - 1 < IMAGES:
                    load_x(i // 2 + O_IMAGES - 1)
            last = i == GROUPS - 1
            scaled, added = i - 2, i - 3
            scalar_tiles = (0, 1) if last else (2, 3)
            no_copies = i >= GROUPS - 1
            if i > 1:
                run(regroup, i + COPY_AHEAD, 0)
            if not no_copies:
                run(root, i - 1)
            if scaled >= 0:
                scale_on_scalar(scaled, scalar_tiles[0])
            if no_copies:
                root(i - 1)
            if no_copies:
                scale_on_scalar(scaled, scalar_tiles[1])
            if i > 1:
                run(add_eps, i - 1)
                run(regroup, i + COPY_AHEAD, 1)
            if scaled >= 0 and not no_copies:
                scale_on_scalar(scaled, scalar_tiles[1])
            if last:
                for j, cols in THROUGH_PSUM:
                    add_x_on_vector(added, j, cols)
                store(added, 0)
                for start, stop in ((PSUM_COLS, 3 * C), (3 * C, 4 * C)):
                    add_x_on_gpsimd(added, start, stop)
                    first = max(1, start // C)
                    store(added, first, stop // C - first)
                lay_x(scaled, 0, C)
            elif added >= 0:
                add_x_on_gpsimd(added, PSUM_COLS, TILES * C)
            for j in range(TILES):
                add_bias(i, j)
                if i == 0 and j == 1:
                    quantise(1, 0)
                    quantise(1, 1)
            for j in range(TILES):
                run(project, i + 1, j)
                if j == TILES - 1:
                    run(transposes, i + COPY_AHEAD + 1, 0)
                square(i, j)
                if i < 2 and j == 0:
                    run(add_eps, i - 1)
                if (i, j) in ((0, 1), (1, 0)):
                    regroup(i + 2, 0)
                    regroup(i + 2, 1)
            run(transposes, i + COPY_AHEAD + 1, 1)
            if last:
                break
            if added >= 0:
                for j, cols in THROUGH_PSUM:
                    add_x_on_vector(added, j, cols)
                store(added)
            if 0 <= added + 1 < LOOP:
                for j, cols in THROUGH_PSUM:
                    lay_x(added + 1, j, cols)
            run(chain, i - 1, 0)
            run(quantise, i + QUANTISE_AHEAD, 0)
            run(chain, i - 1, 1)
            if scaled >= 0:
                scale_on_vector(scaled, 0)
            run(chain, i - 1, 2)
            if scaled >= 0:
                scale_on_vector(scaled, 1)
            run(chain, i - 1, 3)
            run(quantise, i + QUANTISE_AHEAD, 1)

        g = GROUPS - 3
        lay_x(g, 1, C)
        chain(g + 1, 0)
        add_x_on_vector(g, 0, C)
        chain(g + 1, 1)
        add_x_on_vector(g, 1, C)
        store(g, 0, 2)
        chain(g + 1, 2)
        shift_on_vector(g, 2)
        chain(g + 1, 3)
        shift_on_vector(g, 3)
        root(GROUPS - 1)
        shift_on_scalar(g + 1, 1)
        add_eps(GROUPS - 1)
        for j in (2, 3):
            finish(g, j)
            store(g, j)
        for j in (2, 3, 0):
            shift_on_scalar(g + 1, j)
        g += 1
        chain(g + 1, 0)
        finish(g, 1)
        store(g, 1)
        chain(g + 1, 1)
        finish(g, 2)
        store(g, 2)
        chain(g + 1, 2)
        finish(g, 3)
        store(g, 3)
        chain(g + 1, 3)
        for j in (0,):
            finish(g, j)
            store(g, j)
        g += 1
        shift_on_vector(g, 0)
        for j in (1, 2, 3):
            shift_on_scalar(g, j)
        for j in (1, 2, 0, 3):
            finish(g, j)
            store(g, j)
